import numpy as np
import ml_dtypes


def mxq(x, axis, fmt="e4m3"):
    dtype, down = {"e4m3": (ml_dtypes.float8_e4m3fn, 7), "e5m2": (ml_dtypes.float8_e5m2, 14)}[fmt]
    v = np.moveaxis(np.asarray(x, np.float32).astype(ml_dtypes.bfloat16).astype(np.float64), axis, -1)
    blocks = v.reshape(v.shape[:-1] + (-1, 32))
    amax = np.abs(blocks).max(-1, keepdims=True)
    byte = np.maximum(np.where(amax > 0, np.frexp(amax)[1] - 1 + 127, 0) - down, 1)
    scale = np.exp2(byte - 127.0)
    codes = (blocks / scale).astype(np.float32).astype(dtype).astype(np.float64)
    return np.moveaxis((codes * scale).reshape(v.shape), -1, axis)


WIDE = False


def mx_kscale(k):
    if not WIDE:
        return np.ones(k)
    levels = np.array([10, -10, 5, -5, 0])
    a = np.random.permutation(np.resize(levels, k // 512 * 4)).reshape(k // 512, 4)
    idx = np.arange(k)
    return np.exp2(a[idx // 512, idx % 128 // 32])


BF16 = ml_dtypes.bfloat16


def bf(x):
    return np.asarray(x, np.float32).astype(BF16)


def f64(x):
    return np.asarray(x).astype(np.float64)


E2M1 = np.array([0.0, 0.5, 1.0, 1.5, 2.0, 3.0, 4.0, 6.0, -0.0, -0.5, -1.0, -1.5, -2.0, -3.0, -4.0, -6.0])


def pack_weight(w, fmt):
    k, n = w.shape
    w = f64(bf(w)).reshape(k // 32, 32, n)
    amax = np.abs(w).max(1)
    if fmt == "e4m3":
        byte = np.frexp(amax)[1] - 1 + 127 - 7
    else:
        mant, ex = np.frexp(amax / 6.0)
        byte = np.where(mant > 0.5, ex, ex - 1) + 127
    byte = np.clip(np.where(amax > 0, byte, 1), 1, 254)
    scaled = (w * np.exp2(127.0 - byte)[:, None, :]).reshape(k, n).astype(np.float32)
    by_word = np.ascontiguousarray(scaled.reshape(k // 512, 128, 4, n).transpose(0, 1, 3, 2))
    if fmt == "e4m3":
        words = by_word.astype(ml_dtypes.float8_e4m3fn).view(np.uint8)
    else:
        c = by_word.astype(ml_dtypes.float4_e2m1fn).view(np.uint8) & 0xF
        words = c[..., 0::2] | (c[..., 1::2] << 4)
    return np.ascontiguousarray(words), np.ascontiguousarray(byte.astype(np.uint8).reshape(k // 512, 16, n))


def unpack_weight(words, scales, fmt):
    g, p, n, _ = words.shape
    if fmt == "e4m3":
        vals = np.ascontiguousarray(words).view(ml_dtypes.float8_e4m3fn).astype(np.float64)
    else:
        nib = np.empty((g, p, n, 4), np.uint8)
        nib[..., 0::2] = words & 0xF
        nib[..., 1::2] = words >> 4
        vals = E2M1[nib]
    vals = vals * np.repeat(np.exp2(scales.astype(np.float64) - 127.0), 8, axis=1)[..., None]
    return vals.transpose(0, 1, 3, 2).reshape(g * 512, n)

def pack4(w):
    words, scales = pack_weight(w, "e2m1")
    return words.reshape(words.shape[0], 128, -1), scales


def unpack4(words, scales):
    return unpack_weight(words.reshape(words.shape[0], 128, -1, 2), scales, "e2m1")


B, T, D, H, NUM_LAYERS = 4, 256, 512, 512, 3
EPS = 1e-8


def setup_inputs():
    s = mx_kscale(D)
    inv = bf(np.random.standard_normal((B, T, D)) * 0.5 * s)
    Wk = np.random.standard_normal((D, D)) * 2.0 / np.sqrt(D) / s[None, :]
    words, scales = pack4(np.ascontiguousarray(Wk.T))
    bk = bf(2.5 / np.sqrt(D) + 0.7 * np.random.standard_normal(D))
    return {"inv": inv,
            "Wk_words": words,
            "Wk_scales": scales,
            "bk": bk}


def reference(inv, Wk_words, Wk_scales, bk):
    flat = f64(inv).reshape(-1, D)
    out = (mxq(flat, 1, "e4m3") @ unpack4(Wk_words, Wk_scales)) + f64(bk)
    sqrtD = np.sqrt(D)
    S = out.sum(-1, keepdims=True)
    norms = np.sqrt((out * out).sum(-1, keepdims=True))
    c = out * S / (np.maximum(np.abs(out) * sqrtD, EPS) * np.maximum(norms, EPS))
    diff = np.abs(c[1:] - c[:-1]).sum(0)
    return np.broadcast_to(diff, (D, D)).copy()

@@ -1,0 +1,212 @@
+import math
+from contextlib import ExitStack
+
+import concourse.mybir as mybir
+from concourse.masks import make_identity
+
+F32 = mybir.dt.float32
+BF16 = mybir.dt.bfloat16
+I32 = mybir.dt.int32
+U32 = mybir.dt.uint32
+U8 = mybir.dt.uint8
+FP8X4 = mybir.dt.float8_e4m3fn_x4
+FP4X4 = mybir.dt.float4_e2m1fn_x4
+ALU = mybir.AluOpType
+ACT = mybir.ActivationFunctionType
+AXIS = mybir.AxisListType
+
+P = 128
+ROWS = 1024
+D = 512
+EPS = 1e-8
+TILES = ROWS // P
+PAIRS = TILES // 2
+BLOCKS = D // P
+BANK = 512
+CLAMP = EPS / math.sqrt(D)
+
+FLOPS = 2 * ROWS * D * D
+
+
+def tile_dispatcher_pa_s_kernel(tc, inv, Wk_words, Wk_scales, bk, out):
+    nc = tc.nc
+    with ExitStack() as stack:
+        const = stack.enter_context(tc.tile_pool(name="const", bufs=1))
+        keep = stack.enter_context(tc.tile_pool(name="keep", bufs=1))
+        psum_work = stack.enter_context(tc.psum_pool(name="psum_work", bufs=6))
+        psum_hold = stack.enter_context(tc.psum_pool(name="psum_hold", bufs=2))
+
+        w_plane = const.tile([P, D], U8, align_bytes=64)
+        nc.vector.memset(w_plane[:].bitcast(I32), 0)
+        scale_rows = Wk_scales.rearrange("g q n -> (g q) n")
+        for quad in range(4):
+            nc.sync.dma_start(
+                out=w_plane[32 * quad : 32 * quad + 4, :].bitcast(I32),
+                in_=scale_rows[4 * quad : 4 * quad + 4, :].bitcast(I32),
+            )
+        w_bytes = const.tile([P, 2 * D], U8, align_bytes=64)
+        nc.sync.dma_start(
+            out=w_bytes[:].bitcast(I32),
+            in_=Wk_words.rearrange("g p n -> (g p) n").bitcast(I32),
+        )
+        bias_row = const.tile([P, D], BF16)
+        nc.vector.memset(bias_row[:], 0.0)
+        nc.sync.dma_start(out=bias_row[0:1, :], in_=bk.rearrange("(o n) -> o n", o=1))
+
+        rows = inv.flatten_outer_dims().rearrange("(p t) k -> p t k", t=TILES)
+        x_sb = keep.tile([P, TILES, D], BF16)
+        for pair in range(PAIRS):
+            two = slice(2 * pair, 2 * pair + 2)
+            nc.scalar.dma_start(out=x_sb[:, two, :], in_=rows[:, two, :])
+
+        ident = const.tile([P, P], F32)
+        make_identity(nc, ident[:])
+        ones = const.tile([P, P], BF16)
+        nc.gpsimd.memset(ones[:], 1.0)
+        shift_up = const.tile([P, P], F32)
+        nc.vector.memset(shift_up[:], 0.0)
+        nc.vector.tensor_copy(out=shift_up[:, 0 : P - 1], in_=ident[:, 1:P])
+        not_last = const.tile([P, 1], F32)
+        nc.vector.tensor_scalar(
+            out=not_last[:], in0=ident[:, P - 1 : P], scalar1=-1.0, scalar2=1.0,
+            op0=ALU.mult, op1=ALU.add,
+        )
+        one_col = const.tile([P, 1], F32)
+        nc.vector.memset(one_col[:], 1.0)
+        warm = const.tile([P, 1], F32)
+        nc.scalar.activation(out=warm[:], in_=one_col[:], func=ACT.Sqrt)
+
+        bias_ps = psum_hold.tile([P, D], F32, tag="hold")
+        nc.tensor.matmul(out=bias_ps[:], lhsT=ones[:], rhs=bias_row[:], start=True, stop=True)
+        bias_sb = const.tile([P, D], F32)
+        nc.scalar.copy(out=bias_sb[:], in_=bias_ps[:])
+
+        x_words = x_sb[:].rearrange("p t k -> p (t k)").bitcast(F32)
+        grouped = keep.tile([P, TILES * P * 4], BF16, align_bytes=64)
+        grouped_words = grouped[:].bitcast(F32)
+        codes = keep.tile([P, TILES * P], U32, align_bytes=64)
+        planes = keep.tile([P, TILES * P], U8, align_bytes=64)
+        z = keep.tile([P, TILES, D], F32)
+        z_clamped = keep.tile([P, TILES, D], F32)
+        squares = keep.tile([P, TILES, D], F32)
+        row_sum = keep.tile([P, TILES], F32)
+        row_sq = keep.tile([P, TILES], F32)
+
+        for pair in range(PAIRS):
+            flipped = psum_work.tile([P, BANK], F32, tag="work")
+            for a in range(2):
+                t = 2 * pair + a
+                for u in range(2):
+                    nc.tensor.transpose(
+                        flipped[:, (2 * a + u) * P : (2 * a + u + 1) * P],
+                        x_words[:, t * (D // 2) + u : (t + 1) * (D // 2) : 2],
+                        ident[:],
+                    )
+            nc.scalar.copy(
+                out=grouped_words[:, pair * BANK : (pair + 1) * BANK].rearrange(
+                    "q (a r u) -> q a r u", a=2, u=2
+                ),
+                in_=flipped[:].rearrange("q (a u r) -> q a r u", a=2, u=2),
+            )
+            cols = slice(2 * pair * P, (2 * pair + 2) * P)
+            nc.vector.quantize_mx(
+                out=codes[:, cols].bitcast(FP8X4),
+                scales=planes[:, cols],
+                in_=grouped[:, 8 * pair * P : 8 * (pair + 1) * P],
+            )
+            for a in range(2):
+                t = 2 * pair + a
+                acc = psum_work.tile([P, BANK], F32, tag="work")
+                nc.tensor.matmul_mx(
+                    out=acc[:],
+                    lhsT=codes[:, t * P : (t + 1) * P].bitcast(FP8X4),
+                    lhsT_scale=planes[:, t * P : (t + 1) * P],
+                    rhs=w_bytes[:].bitcast(FP4X4),
+                    rhs_scale=w_plane[:],
+                    start=True,
+                    stop=True,
+                )
+                nc.vector.scalar_tensor_tensor(
+                    out=z[:, t, :], in0=acc[:], scalar=1.0, in1=bias_sb[:],
+                    op0=ALU.mult, op1=ALU.add, accum_out=row_sum[:, t : t + 1],
+                )
+                nc.scalar.activation(
+                    out=squares[:, t, :], in_=z[:, t, :], func=ACT.Square,
+                    accum_out=row_sq[:, t : t + 1],
+                )
+            two = slice(2 * pair, 2 * pair + 2)
+            nc.vector.tensor_scalar(
+                out=z_clamped[:, two, :], in0=z[:, two, :], scalar1=CLAMP, scalar2=-CLAMP,
+                op0=ALU.min, op1=ALU.max,
+            )
+
+        sq_floor = keep.tile([P, TILES], F32)
+        nc.vector.tensor_scalar_max(out=sq_floor[:], in0=row_sq[:], scalar1=EPS * EPS)
+        denom = keep.tile([P, TILES], F32)
+        nc.scalar.activation(out=denom[:], in_=sq_floor[:], func=ACT.Sqrt, scale=EPS * EPS)
+        inv_denom = keep.tile([P, TILES], F32)
+        nc.vector.reciprocal(out=inv_denom[:], in_=denom[:])
+        gain = keep.tile([P, TILES + 1], F32)
+        nc.vector.tensor_mul(out=gain[:, 0:TILES], in0=inv_denom[:], in1=row_sum[:])
+        nc.vector.tensor_mul(
+            out=gain[:, TILES : TILES + 1], in0=gain[:, TILES - 1 : TILES], in1=not_last[:]
+        )
+
+        c_even = keep.tile([P, PAIRS, D], F32)
+        for pair in range(PAIRS):
+            nc.vector.tensor_scalar_mul(
+                out=c_even[:, pair, :], in0=z_clamped[:, 2 * pair, :],
+                scalar1=gain[:, 2 * pair : 2 * pair + 1],
+            )
+        c_next = psum_hold.tile([P, D], F32, tag="hold")
+        nc.tensor.matmul(out=c_next[:], lhsT=shift_up[:], rhs=c_even[:, 0, :], start=True, stop=True)
+
+        delta = keep.tile([P, TILES, D], F32)
+        abs_delta = keep.tile([P, PAIRS, BLOCKS, 2 * P], F32)
+        partial = keep.tile([P, BLOCKS, PAIRS], F32)
+        for pair in range(PAIRS):
+            t = 2 * pair + 1
+            last = pair == PAIRS - 1
+            nc.vector.scalar_tensor_tensor(
+                out=delta[:, t - 1, :], in0=z_clamped[:, t, :], scalar=gain[:, t : t + 1],
+                in1=c_even[:, pair, :], op0=ALU.mult, op1=ALU.subtract,
+            )
+            nc.vector.scalar_tensor_tensor(
+                out=delta[:, t, :], in0=z_clamped[:, t, :],
+                scalar=gain[:, TILES : TILES + 1] if last else gain[:, t : t + 1],
+                in1=c_next[:] if last else c_even[:, pair + 1, :],
+                op0=ALU.mult, op1=ALU.subtract,
+            )
+            for half in range(2):
+                flipped = psum_work.tile([P, BANK], F32, tag="work")
+                for b in range(2):
+                    block = 2 * half + b
+                    for a in range(2):
+                        nc.tensor.transpose(
+                            flipped[:, (2 * b + a) * P : (2 * b + a + 1) * P],
+                            delta[:, t - 1 + a, block * P : (block + 1) * P],
+                            ident[:],
+                        )
+                for b in range(2):
+                    block = 2 * half + b
+                    nc.scalar.activation(
+                        out=abs_delta[:, pair, block, :],
+                        in_=flipped[:, 2 * b * P : 2 * (b + 1) * P],
+                        func=ACT.Abs,
+                        accum_out=partial[:, block, pair : pair + 1],
+                    )
+
+        diff_col = keep.tile([P, BLOCKS], F32)
+        nc.vector.tensor_reduce(out=diff_col[:], in_=partial[:], axis=AXIS.X, op=ALU.add)
+        spread = psum_hold.tile([P, D], F32, tag="hold")
+        for block in range(BLOCKS):
+            nc.tensor.transpose(
+                spread[:, block * P : (block + 1) * P],
+                diff_col[:, block : block + 1].to_broadcast([P, P]),
+                ident[:],
+            )
+        out_sb = keep.tile([P, D], F32)
+        nc.vector.tensor_copy(out=out_sb[:], in_=spread[:])
+        for e in range(D // P):
+            queue = nc.sync if e % 2 == 0 else nc.scalar
+            queue.dma_start(out=out[e * P : (e + 1) * P, :], in_=out_sb[:])

@@ -24,6 +24,13 @@ PAIRS = TILES // 2
 BLOCKS = D // P
 BANK = 512
 CLAMP = EPS / math.sqrt(D)
+SHRINK = 2.0 ** -32
+
+FLIP_LEAD = 3
+QUANT_LEAD = 2
+GAIN_LAG = 2
+DIFF_LAG = 3
+SUM_LAG = 4
 
 FLOPS = 2 * ROWS * D * D
 
@@ -35,7 +42,16 @@ def tile_dispatcher_pa_s_kernel(tc, inv, Wk_words, Wk_scales, bk, out):
         keep = stack.enter_context(tc.tile_pool(name="keep", bufs=1))
         psum_work = stack.enter_context(tc.psum_pool(name="psum_work", bufs=6))
         psum_hold = stack.enter_context(tc.psum_pool(name="psum_hold", bufs=2))
+        stack.enter_context(tc.manual_schedule())
 
+        rows = inv.flatten_outer_dims().rearrange("(p t) k -> p t k", t=TILES)
+        x_sb = keep.tile([P, TILES, D], BF16)
+
+        def load_pair(c):
+            nc.sync.dma_start(out=x_sb[:, 2 * c : 2 * c + 2, :], in_=rows[:, 2 * c : 2 * c + 2, :])
+
+        load_pair(0)
+        load_pair(1)
         w_plane = const.tile([P, D], U8, align_bytes=64)
         nc.vector.memset(w_plane[:].bitcast(I32), 0)
         scale_rows = Wk_scales.rearrange("g q n -> (g q) n")
@@ -49,20 +65,20 @@ def tile_dispatcher_pa_s_kernel(tc, inv, Wk_words, Wk_scales, bk, out):
             out=w_bytes[:].bitcast(I32),
             in_=Wk_words.rearrange("g p n -> (g p) n").bitcast(I32),
         )
-        bias_row = const.tile([P, D], BF16)
-        nc.vector.memset(bias_row[:], 0.0)
-        nc.sync.dma_start(out=bias_row[0:1, :], in_=bk.rearrange("(o n) -> o n", o=1))
-
-        rows = inv.flatten_outer_dims().rearrange("(p t) k -> p t k", t=TILES)
-        x_sb = keep.tile([P, TILES, D], BF16)
-        for pair in range(PAIRS):
-            two = slice(2 * pair, 2 * pair + 2)
-            nc.scalar.dma_start(out=x_sb[:, two, :], in_=rows[:, two, :])
+        load_pair(2)
+        load_pair(3)
 
         ident = const.tile([P, P], F32)
         make_identity(nc, ident[:])
         ones = const.tile([P, P], BF16)
         nc.gpsimd.memset(ones[:], 1.0)
+        bias_row = const.tile([P, D], BF16)
+        nc.vector.memset(bias_row[:], 0.0)
+        nc.gpsimd.dma_start(out=bias_row[0:1, :], in_=bk.rearrange("(o n) -> o n", o=1))
+        minus_eps2 = const.tile([P, 1], F32)
+        nc.vector.memset(minus_eps2[:], -EPS * EPS)
+        eps2_shrunk = const.tile([P, 1], F32)
+        nc.vector.memset(eps2_shrunk[:], SHRINK * EPS * EPS)
         shift_up = const.tile([P, P], F32)
         nc.vector.memset(shift_up[:], 0.0)
         nc.vector.tensor_copy(out=shift_up[:, 0 : P - 1], in_=ident[:, 1:P])
@@ -71,31 +87,35 @@ def tile_dispatcher_pa_s_kernel(tc, inv, Wk_words, Wk_scales, bk, out):
             out=not_last[:], in0=ident[:, P - 1 : P], scalar1=-1.0, scalar2=1.0,
             op0=ALU.mult, op1=ALU.add,
         )
-        one_col = const.tile([P, 1], F32)
-        nc.vector.memset(one_col[:], 1.0)
         warm = const.tile([P, 1], F32)
-        nc.scalar.activation(out=warm[:], in_=one_col[:], func=ACT.Sqrt)
-
-        bias_ps = psum_hold.tile([P, D], F32, tag="hold")
-        nc.tensor.matmul(out=bias_ps[:], lhsT=ones[:], rhs=bias_row[:], start=True, stop=True)
-        bias_sb = const.tile([P, D], F32)
-        nc.scalar.copy(out=bias_sb[:], in_=bias_ps[:])
+        nc.scalar.activation(out=warm[:], in_=eps2_shrunk[:], func=ACT.Abs_reciprocal_sqrt)
 
         x_words = x_sb[:].rearrange("p t k -> p (t k)").bitcast(F32)
         grouped = keep.tile([P, TILES * P * 4], BF16, align_bytes=64)
         grouped_words = grouped[:].bitcast(F32)
         codes = keep.tile([P, TILES * P], U32, align_bytes=64)
         planes = keep.tile([P, TILES * P], U8, align_bytes=64)
+        bias_sb = const.tile([P, D], F32)
         z = keep.tile([P, TILES, D], F32)
         z_clamped = keep.tile([P, TILES, D], F32)
         squares = keep.tile([P, TILES, D], F32)
         row_sum = keep.tile([P, TILES], F32)
         row_sq = keep.tile([P, TILES], F32)
+        sq_excess = keep.tile([P, TILES], F32)
+        inv_denom = keep.tile([P, TILES], F32)
+        gain = keep.tile([P, TILES + 1], F32)
+        c_even = keep.tile([P, PAIRS, D], F32)
+        delta = keep.tile([P, TILES, D], F32)
+        abs_delta = keep.tile([P, PAIRS, BLOCKS, 2 * P], F32)
+        partial = keep.tile([P, BLOCKS, PAIRS], F32)
+        acc = {}
+        turned = {}
+        c_next = psum_hold.tile([P, D], F32, tag="hold", name="c_next")
 
-        for pair in range(PAIRS):
-            flipped = psum_work.tile([P, BANK], F32, tag="work")
+        def flip(c):
+            flipped = psum_work.tile([P, BANK], F32, tag="work", name="flipped")
             for a in range(2):
-                t = 2 * pair + a
+                t = 2 * c + a
                 for u in range(2):
                     nc.tensor.transpose(
                         flipped[:, (2 * a + u) * P : (2 * a + u + 1) * P],
@@ -103,22 +123,30 @@ def tile_dispatcher_pa_s_kernel(tc, inv, Wk_words, Wk_scales, bk, out):
                         ident[:],
                     )
             nc.scalar.copy(
-                out=grouped_words[:, pair * BANK : (pair + 1) * BANK].rearrange(
+                out=grouped_words[:, c * BANK : (c + 1) * BANK].rearrange(
                     "q (a r u) -> q a r u", a=2, u=2
                 ),
                 in_=flipped[:].rearrange("q (a u r) -> q a r u", a=2, u=2),
             )
-            cols = slice(2 * pair * P, (2 * pair + 2) * P)
+
+        def quantise(c):
+            cols = slice(2 * c * P, (2 * c + 2) * P)
             nc.vector.quantize_mx(
                 out=codes[:, cols].bitcast(FP8X4),
                 scales=planes[:, cols],
-                in_=grouped[:, 8 * pair * P : 8 * (pair + 1) * P],
+                in_=grouped[:, 8 * c * P : 8 * (c + 1) * P],
             )
-            for a in range(2):
-                t = 2 * pair + a
-                acc = psum_work.tile([P, BANK], F32, tag="work")
+
+        def spread_bias():
+            bias_ps = psum_hold.tile([P, D], F32, tag="hold", name="bias_ps")
+            nc.tensor.matmul(out=bias_ps[:], lhsT=ones[:], rhs=bias_row[:], start=True, stop=True)
+            nc.scalar.copy(out=bias_sb[:], in_=bias_ps[:])
+
+        def product(c):
+            for t in (2 * c, 2 * c + 1):
+                acc[t] = psum_work.tile([P, BANK], F32, tag="work", name="acc")
                 nc.tensor.matmul_mx(
-                    out=acc[:],
+                    out=acc[t][:],
                     lhsT=codes[:, t * P : (t + 1) * P].bitcast(FP8X4),
                     lhsT_scale=planes[:, t * P : (t + 1) * P],
                     rhs=w_bytes[:].bitcast(FP4X4),
@@ -126,87 +154,120 @@ def tile_dispatcher_pa_s_kernel(tc, inv, Wk_words, Wk_scales, bk, out):
                     start=True,
                     stop=True,
                 )
+
+        def row_work(c):
+            two = slice(2 * c, 2 * c + 2)
+            for t in (2 * c, 2 * c + 1):
                 nc.vector.scalar_tensor_tensor(
-                    out=z[:, t, :], in0=acc[:], scalar=1.0, in1=bias_sb[:],
+                    out=z[:, t, :], in0=acc[t][:], scalar=1.0, in1=bias_sb[:],
                     op0=ALU.mult, op1=ALU.add, accum_out=row_sum[:, t : t + 1],
                 )
                 nc.scalar.activation(
                     out=squares[:, t, :], in_=z[:, t, :], func=ACT.Square,
                     accum_out=row_sq[:, t : t + 1],
                 )
-            two = slice(2 * pair, 2 * pair + 2)
             nc.vector.tensor_scalar(
                 out=z_clamped[:, two, :], in0=z[:, two, :], scalar1=CLAMP, scalar2=-CLAMP,
                 op0=ALU.min, op1=ALU.max,
             )
-
-        sq_floor = keep.tile([P, TILES], F32)
-        nc.vector.tensor_scalar_max(out=sq_floor[:], in0=row_sq[:], scalar1=EPS * EPS)
-        denom = keep.tile([P, TILES], F32)
-        nc.scalar.activation(out=denom[:], in_=sq_floor[:], func=ACT.Sqrt, scale=EPS * EPS)
-        inv_denom = keep.tile([P, TILES], F32)
-        nc.vector.reciprocal(out=inv_denom[:], in_=denom[:])
-        gain = keep.tile([P, TILES + 1], F32)
-        nc.vector.tensor_mul(out=gain[:, 0:TILES], in0=inv_denom[:], in1=row_sum[:])
-        nc.vector.tensor_mul(
-            out=gain[:, TILES : TILES + 1], in0=gain[:, TILES - 1 : TILES], in1=not_last[:]
-        )
-
-        c_even = keep.tile([P, PAIRS, D], F32)
-        for pair in range(PAIRS):
-            nc.vector.tensor_scalar_mul(
-                out=c_even[:, pair, :], in0=z_clamped[:, 2 * pair, :],
-                scalar1=gain[:, 2 * pair : 2 * pair + 1],
+            nc.scalar.activation(
+                out=sq_excess[:, two], in_=row_sq[:, two], func=ACT.Relu, bias=minus_eps2[:]
             )
-        c_next = psum_hold.tile([P, D], F32, tag="hold")
-        nc.tensor.matmul(out=c_next[:], lhsT=shift_up[:], rhs=c_even[:, 0, :], start=True, stop=True)
+            nc.scalar.activation(
+                out=inv_denom[:, two], in_=sq_excess[:, two], func=ACT.Abs_reciprocal_sqrt,
+                scale=SHRINK, bias=eps2_shrunk[:],
+            )
 
-        delta = keep.tile([P, TILES, D], F32)
-        abs_delta = keep.tile([P, PAIRS, BLOCKS, 2 * P], F32)
-        partial = keep.tile([P, BLOCKS, PAIRS], F32)
-        for pair in range(PAIRS):
-            t = 2 * pair + 1
-            last = pair == PAIRS - 1
+        def gains(c):
+            two = slice(2 * c, 2 * c + 2)
+            nc.vector.scalar_tensor_tensor(
+                out=gain[:, two], in0=inv_denom[:, two], scalar=math.sqrt(SHRINK) / EPS,
+                in1=row_sum[:, two], op0=ALU.mult, op1=ALU.mult,
+            )
+            nc.vector.tensor_scalar_mul(
+                out=c_even[:, c, :], in0=z_clamped[:, 2 * c, :], scalar1=gain[:, 2 * c : 2 * c + 1]
+            )
+
+        def differences(c):
+            t = 2 * c + 1
+            last = c == PAIRS - 1
+            if last:
+                nc.vector.tensor_mul(
+                    out=gain[:, TILES : TILES + 1], in0=gain[:, t : t + 1], in1=not_last[:]
+                )
             nc.vector.scalar_tensor_tensor(
                 out=delta[:, t - 1, :], in0=z_clamped[:, t, :], scalar=gain[:, t : t + 1],
-                in1=c_even[:, pair, :], op0=ALU.mult, op1=ALU.subtract,
+                in1=c_even[:, c, :], op0=ALU.mult, op1=ALU.subtract,
             )
             nc.vector.scalar_tensor_tensor(
                 out=delta[:, t, :], in0=z_clamped[:, t, :],
                 scalar=gain[:, TILES : TILES + 1] if last else gain[:, t : t + 1],
-                in1=c_next[:] if last else c_even[:, pair + 1, :],
+                in1=c_next[:] if last else c_even[:, c + 1, :],
                 op0=ALU.mult, op1=ALU.subtract,
             )
             for half in range(2):
-                flipped = psum_work.tile([P, BANK], F32, tag="work")
+                turned[c, half] = psum_work.tile([P, BANK], F32, tag="work", name="turned")
                 for b in range(2):
                     block = 2 * half + b
                     for a in range(2):
                         nc.tensor.transpose(
-                            flipped[:, (2 * b + a) * P : (2 * b + a + 1) * P],
+                            turned[c, half][:, (2 * b + a) * P : (2 * b + a + 1) * P],
                             delta[:, t - 1 + a, block * P : (block + 1) * P],
                             ident[:],
                         )
-                for b in range(2):
-                    block = 2 * half + b
-                    nc.scalar.activation(
-                        out=abs_delta[:, pair, block, :],
-                        in_=flipped[:, 2 * b * P : 2 * (b + 1) * P],
-                        func=ACT.Abs,
-                        accum_out=partial[:, block, pair : pair + 1],
-                    )
+
+        def sums(c):
+            for block in range(BLOCKS):
+                half, b = divmod(block, 2)
+                nc.scalar.activation(
+                    out=abs_delta[:, c, block, :],
+                    in_=turned[c, half][:, 2 * b * P : 2 * (b + 1) * P],
+                    func=ACT.Abs,
+                    accum_out=partial[:, block, c : c + 1],
+                )
+
+        flip(0)
+        quantise(0)
+        flip(1)
+        quantise(1)
+        spread_bias()
+        flip(2)
+        for s in range(PAIRS + SUM_LAG):
+            if s < PAIRS:
+                product(s)
+            if s == PAIRS - 1:
+                nc.tensor.matmul(
+                    out=c_next[:], lhsT=shift_up[:], rhs=c_even[:, 0, :], start=True, stop=True
+                )
+            if 0 <= s - SUM_LAG < PAIRS:
+                sums(s - SUM_LAG)
+            if 0 <= s - GAIN_LAG < PAIRS:
+                gains(s - GAIN_LAG)
+            if 0 <= s - DIFF_LAG < PAIRS:
+                differences(s - DIFF_LAG)
+            if s < PAIRS:
+                row_work(s)
+            if s + QUANT_LEAD < PAIRS:
+                quantise(s + QUANT_LEAD)
+            if s + FLIP_LEAD < PAIRS:
+                flip(s + FLIP_LEAD)
 
         diff_col = keep.tile([P, BLOCKS], F32)
         nc.vector.tensor_reduce(out=diff_col[:], in_=partial[:], axis=AXIS.X, op=ALU.add)
-        spread = psum_hold.tile([P, D], F32, tag="hold")
-        for block in range(BLOCKS):
-            nc.tensor.transpose(
-                spread[:, block * P : (block + 1) * P],
-                diff_col[:, block : block + 1].to_broadcast([P, P]),
-                ident[:],
-            )
         out_sb = keep.tile([P, D], F32)
-        nc.vector.tensor_copy(out=out_sb[:], in_=spread[:])
+        for half in range(2):
+            spread = psum_hold.tile([P, D // 2], F32, tag="hold", name="spread")
+            for b in range(2):
+                block = 2 * half + b
+                nc.tensor.transpose(
+                    spread[:, b * P : (b + 1) * P],
+                    diff_col[:, block : block + 1].to_broadcast([P, P]),
+                    ident[:],
+                )
+            if half == 0:
+                nc.vector.tensor_copy(out=out_sb[:, 0 : D // 2], in_=spread[:])
+            else:
+                nc.scalar.copy(out=out_sb[:, D // 2 : D], in_=spread[:])
         for e in range(D // P):
             queue = nc.sync if e % 2 == 0 else nc.scalar
             queue.dma_start(out=out[e * P : (e + 1) * P, :], in_=out_sb[:])

@@ -26,8 +26,7 @@ BANK = 512
 CLAMP = EPS / math.sqrt(D)
 SHRINK = 2.0 ** -32
 
-FLIP_LEAD = 3
-QUANT_LEAD = 2
+FLIP_LEAD = 2
 GAIN_LAG = 2
 DIFF_LAG = 3
 SUM_LAG = 4
@@ -42,7 +41,6 @@ def tile_dispatcher_pa_s_kernel(tc, inv, Wk_words, Wk_scales, bk, out):
         keep = stack.enter_context(tc.tile_pool(name="keep", bufs=1))
         psum_work = stack.enter_context(tc.psum_pool(name="psum_work", bufs=6))
         psum_hold = stack.enter_context(tc.psum_pool(name="psum_hold", bufs=2))
-        stack.enter_context(tc.manual_schedule())
 
         rows = inv.flatten_outer_dims().rearrange("(p t) k -> p t k", t=TILES)
         x_sb = keep.tile([P, TILES, D], BF16)
@@ -52,6 +50,14 @@ def tile_dispatcher_pa_s_kernel(tc, inv, Wk_words, Wk_scales, bk, out):
 
         load_pair(0)
         load_pair(1)
+        bias_row = const.tile([P, D], BF16)
+        nc.gpsimd.memset(bias_row[:], 0.0)
+        nc.scalar.dma_start(out=bias_row[0:1, :], in_=bk.rearrange("(o n) -> o n", o=1))
+        w_bytes = const.tile([P, 2 * D], U8, align_bytes=64)
+        nc.sync.dma_start(
+            out=w_bytes[:].bitcast(I32),
+            in_=Wk_words.rearrange("g p n -> (g p) n").bitcast(I32),
+        )
         w_plane = const.tile([P, D], U8, align_bytes=64)
         nc.vector.memset(w_plane[:].bitcast(I32), 0)
         scale_rows = Wk_scales.rearrange("g q n -> (g q) n")
@@ -60,11 +66,6 @@ def tile_dispatcher_pa_s_kernel(tc, inv, Wk_words, Wk_scales, bk, out):
                 out=w_plane[32 * quad : 32 * quad + 4, :].bitcast(I32),
                 in_=scale_rows[4 * quad : 4 * quad + 4, :].bitcast(I32),
             )
-        w_bytes = const.tile([P, 2 * D], U8, align_bytes=64)
-        nc.sync.dma_start(
-            out=w_bytes[:].bitcast(I32),
-            in_=Wk_words.rearrange("g p n -> (g p) n").bitcast(I32),
-        )
         load_pair(2)
         load_pair(3)
 
@@ -72,9 +73,6 @@ def tile_dispatcher_pa_s_kernel(tc, inv, Wk_words, Wk_scales, bk, out):
         make_identity(nc, ident[:])
         ones = const.tile([P, P], BF16)
         nc.gpsimd.memset(ones[:], 1.0)
-        bias_row = const.tile([P, D], BF16)
-        nc.vector.memset(bias_row[:], 0.0)
-        nc.gpsimd.dma_start(out=bias_row[0:1, :], in_=bk.rearrange("(o n) -> o n", o=1))
         minus_eps2 = const.tile([P, 1], F32)
         nc.vector.memset(minus_eps2[:], -EPS * EPS)
         eps2_shrunk = const.tile([P, 1], F32)
@@ -195,26 +193,23 @@ def tile_dispatcher_pa_s_kernel(tc, inv, Wk_words, Wk_scales, bk, out):
                 nc.vector.tensor_mul(
                     out=gain[:, TILES : TILES + 1], in0=gain[:, t : t + 1], in1=not_last[:]
                 )
-            nc.vector.scalar_tensor_tensor(
-                out=delta[:, t - 1, :], in0=z_clamped[:, t, :], scalar=gain[:, t : t + 1],
-                in1=c_even[:, c, :], op0=ALU.mult, op1=ALU.subtract,
-            )
-            nc.vector.scalar_tensor_tensor(
-                out=delta[:, t, :], in0=z_clamped[:, t, :],
-                scalar=gain[:, TILES : TILES + 1] if last else gain[:, t : t + 1],
-                in1=c_next[:] if last else c_even[:, c + 1, :],
-                op0=ALU.mult, op1=ALU.subtract,
-            )
             for half in range(2):
                 turned[c, half] = psum_work.tile([P, BANK], F32, tag="work", name="turned")
-                for b in range(2):
-                    block = 2 * half + b
-                    for a in range(2):
-                        nc.tensor.transpose(
-                            turned[c, half][:, (2 * b + a) * P : (2 * b + a + 1) * P],
-                            delta[:, t - 1 + a, block * P : (block + 1) * P],
-                            ident[:],
-                        )
+            for a in range(2):
+                to_next = last and a == 1
+                nc.vector.scalar_tensor_tensor(
+                    out=delta[:, t - 1 + a, :], in0=z_clamped[:, t, :],
+                    scalar=gain[:, TILES : TILES + 1] if to_next else gain[:, t : t + 1],
+                    in1=c_next[:] if to_next else c_even[:, c + a, :],
+                    op0=ALU.mult, op1=ALU.subtract,
+                )
+                for block in range(BLOCKS):
+                    half, b = divmod(block, 2)
+                    nc.tensor.transpose(
+                        turned[c, half][:, (2 * b + a) * P : (2 * b + a + 1) * P],
+                        delta[:, t - 1 + a, block * P : (block + 1) * P],
+                        ident[:],
+                    )
 
         def sums(c):
             for block in range(BLOCKS):
@@ -231,10 +226,11 @@ def tile_dispatcher_pa_s_kernel(tc, inv, Wk_words, Wk_scales, bk, out):
         flip(1)
         quantise(1)
         spread_bias()
-        flip(2)
         for s in range(PAIRS + SUM_LAG):
             if s < PAIRS:
                 product(s)
+            if s + FLIP_LEAD < PAIRS:
+                flip(s + FLIP_LEAD)
             if s == PAIRS - 1:
                 nc.tensor.matmul(
                     out=c_next[:], lhsT=shift_up[:], rhs=c_even[:, 0, :], start=True, stop=True
@@ -247,10 +243,8 @@ def tile_dispatcher_pa_s_kernel(tc, inv, Wk_words, Wk_scales, bk, out):
                 differences(s - DIFF_LAG)
             if s < PAIRS:
                 row_work(s)
-            if s + QUANT_LEAD < PAIRS:
-                quantise(s + QUANT_LEAD)
             if s + FLIP_LEAD < PAIRS:
-                flip(s + FLIP_LEAD)
+                quantise(s + FLIP_LEAD)
 
         diff_col = keep.tile([P, BLOCKS], F32)
         nc.vector.tensor_reduce(out=diff_col[:], in_=partial[:], axis=AXIS.X, op=ALU.add)

@@ -27,6 +27,8 @@ CLAMP = EPS / math.sqrt(D)
 SHRINK = 2.0 ** -32
 
 FLIP_LEAD = 2
+PRODUCT_LEAD = 1
+CLAMP_LAG = 1
 GAIN_LAG = 2
 DIFF_LAG = 3
 SUM_LAG = 4
@@ -41,6 +43,7 @@ def tile_dispatcher_pa_s_kernel(tc, inv, Wk_words, Wk_scales, bk, out):
         keep = stack.enter_context(tc.tile_pool(name="keep", bufs=1))
         psum_work = stack.enter_context(tc.psum_pool(name="psum_work", bufs=6))
         psum_hold = stack.enter_context(tc.psum_pool(name="psum_hold", bufs=2))
+        stack.enter_context(tc.manual_schedule())
 
         rows = inv.flatten_outer_dims().rearrange("(p t) k -> p t k", t=TILES)
         x_sb = keep.tile([P, TILES, D], BF16)
@@ -153,21 +156,18 @@ def tile_dispatcher_pa_s_kernel(tc, inv, Wk_words, Wk_scales, bk, out):
                     stop=True,
                 )
 
-        def row_work(c):
-            two = slice(2 * c, 2 * c + 2)
-            for t in (2 * c, 2 * c + 1):
-                nc.vector.scalar_tensor_tensor(
-                    out=z[:, t, :], in0=acc[t][:], scalar=1.0, in1=bias_sb[:],
-                    op0=ALU.mult, op1=ALU.add, accum_out=row_sum[:, t : t + 1],
-                )
-                nc.scalar.activation(
-                    out=squares[:, t, :], in_=z[:, t, :], func=ACT.Square,
-                    accum_out=row_sq[:, t : t + 1],
-                )
-            nc.vector.tensor_scalar(
-                out=z_clamped[:, two, :], in0=z[:, two, :], scalar1=CLAMP, scalar2=-CLAMP,
-                op0=ALU.min, op1=ALU.max,
+        def add_bias(t):
+            nc.vector.scalar_tensor_tensor(
+                out=z[:, t, :], in0=acc[t][:], scalar=1.0, in1=bias_sb[:],
+                op0=ALU.mult, op1=ALU.add, accum_out=row_sum[:, t : t + 1],
             )
+            nc.scalar.activation(
+                out=squares[:, t, :], in_=z[:, t, :], func=ACT.Square,
+                accum_out=row_sq[:, t : t + 1],
+            )
+
+        def inverse_norm(c):
+            two = slice(2 * c, 2 * c + 2)
             nc.scalar.activation(
                 out=sq_excess[:, two], in_=row_sq[:, two], func=ACT.Relu, bias=minus_eps2[:]
             )
@@ -176,12 +176,21 @@ def tile_dispatcher_pa_s_kernel(tc, inv, Wk_words, Wk_scales, bk, out):
                 scale=SHRINK, bias=eps2_shrunk[:],
             )
 
-        def gains(c):
+        def clamp(c):
+            two = slice(2 * c, 2 * c + 2)
+            nc.vector.tensor_scalar(
+                out=z_clamped[:, two, :], in0=z[:, two, :], scalar1=CLAMP, scalar2=-CLAMP,
+                op0=ALU.min, op1=ALU.max,
+            )
+
+        def row_gain(c):
             two = slice(2 * c, 2 * c + 2)
             nc.vector.scalar_tensor_tensor(
                 out=gain[:, two], in0=inv_denom[:, two], scalar=math.sqrt(SHRINK) / EPS,
                 in1=row_sum[:, two], op0=ALU.mult, op1=ALU.mult,
             )
+
+        def scale_even(c):
             nc.vector.tensor_scalar_mul(
                 out=c_even[:, c, :], in0=z_clamped[:, 2 * c, :], scalar1=gain[:, 2 * c : 2 * c + 1]
             )
@@ -221,30 +230,41 @@ def tile_dispatcher_pa_s_kernel(tc, inv, Wk_words, Wk_scales, bk, out):
                     accum_out=partial[:, block, c : c + 1],
                 )
 
+        def pairs_at(s):
+            return [s] if 0 <= s < PAIRS else []
+
         flip(0)
         quantise(0)
         flip(1)
         quantise(1)
         spread_bias()
+        product(0)
         for s in range(PAIRS + SUM_LAG):
-            if s < PAIRS:
-                product(s)
-            if s + FLIP_LEAD < PAIRS:
-                flip(s + FLIP_LEAD)
+            for c in pairs_at(s + FLIP_LEAD):
+                flip(c)
+            for c in pairs_at(s + PRODUCT_LEAD):
+                product(c)
             if s == PAIRS - 1:
                 nc.tensor.matmul(
                     out=c_next[:], lhsT=shift_up[:], rhs=c_even[:, 0, :], start=True, stop=True
                 )
-            if 0 <= s - SUM_LAG < PAIRS:
-                sums(s - SUM_LAG)
-            if 0 <= s - GAIN_LAG < PAIRS:
-                gains(s - GAIN_LAG)
-            if 0 <= s - DIFF_LAG < PAIRS:
-                differences(s - DIFF_LAG)
-            if s < PAIRS:
-                row_work(s)
-            if s + FLIP_LEAD < PAIRS:
-                quantise(s + FLIP_LEAD)
+            for c in pairs_at(s - SUM_LAG):
+                sums(c)
+            for c in pairs_at(s - GAIN_LAG):
+                row_gain(c)
+            for c in pairs_at(s):
+                add_bias(2 * c)
+            for c in pairs_at(s - CLAMP_LAG):
+                clamp(c)
+            for c in pairs_at(s):
+                add_bias(2 * c + 1)
+                inverse_norm(c)
+            for c in pairs_at(s - GAIN_LAG):
+                scale_even(c)
+            for c in pairs_at(s - DIFF_LAG):
+                differences(c)
+            for c in pairs_at(s + FLIP_LEAD):
+                quantise(c)
 
         diff_col = keep.tile([P, BLOCKS], F32)
         nc.vector.tensor_reduce(out=diff_col[:], in_=partial[:], axis=AXIS.X, op=ALU.add)
@@ -263,5 +283,4 @@ def tile_dispatcher_pa_s_kernel(tc, inv, Wk_words, Wk_scales, bk, out):
             else:
                 nc.scalar.copy(out=out_sb[:, D // 2 : D], in_=spread[:])
         for e in range(D // P):
-            queue = nc.sync if e % 2 == 0 else nc.scalar
-            queue.dma_start(out=out[e * P : (e + 1) * P, :], in_=out_sb[:])
+            nc.sync.dma_start(out=out[e * P : (e + 1) * P, :], in_=out_sb[:])

@@ -51,16 +51,11 @@ def tile_dispatcher_pa_s_kernel(tc, inv, Wk_words, Wk_scales, bk, out):
         def load_pair(c):
             nc.sync.dma_start(out=x_sb[:, 2 * c : 2 * c + 2, :], in_=rows[:, 2 * c : 2 * c + 2, :])
 
-        load_pair(0)
-        load_pair(1)
         bias_row = const.tile([P, D], BF16)
         nc.gpsimd.memset(bias_row[:], 0.0)
         nc.scalar.dma_start(out=bias_row[0:1, :], in_=bk.rearrange("(o n) -> o n", o=1))
-        w_bytes = const.tile([P, 2 * D], U8, align_bytes=64)
-        nc.sync.dma_start(
-            out=w_bytes[:].bitcast(I32),
-            in_=Wk_words.rearrange("g p n -> (g p) n").bitcast(I32),
-        )
+        load_pair(0)
+        load_pair(1)
         w_plane = const.tile([P, D], U8, align_bytes=64)
         nc.vector.memset(w_plane[:].bitcast(I32), 0)
         scale_rows = Wk_scales.rearrange("g q n -> (g q) n")
@@ -69,6 +64,11 @@ def tile_dispatcher_pa_s_kernel(tc, inv, Wk_words, Wk_scales, bk, out):
                 out=w_plane[32 * quad : 32 * quad + 4, :].bitcast(I32),
                 in_=scale_rows[4 * quad : 4 * quad + 4, :].bitcast(I32),
             )
+        w_bytes = const.tile([P, 2 * D], U8, align_bytes=64)
+        nc.sync.dma_start(
+            out=w_bytes[:].bitcast(I32),
+            in_=Wk_words.rearrange("g p n -> (g p) n").bitcast(I32),
+        )
         load_pair(2)
         load_pair(3)
 
@@ -113,10 +113,10 @@ def tile_dispatcher_pa_s_kernel(tc, inv, Wk_words, Wk_scales, bk, out):
         turned = {}
         c_next = psum_hold.tile([P, D], F32, tag="hold", name="c_next")
 
-        def flip(c):
-            flipped = psum_work.tile([P, BANK], F32, tag="work", name="flipped")
-            for a in range(2):
-                t = 2 * c + a
+        def flip(first, count):
+            flipped = psum_work.tile([P, count * 2 * P], F32, tag="work", name="flipped")
+            for a in range(count):
+                t = first + a
                 for u in range(2):
                     nc.tensor.transpose(
                         flipped[:, (2 * a + u) * P : (2 * a + u + 1) * P],
@@ -124,18 +124,18 @@ def tile_dispatcher_pa_s_kernel(tc, inv, Wk_words, Wk_scales, bk, out):
                         ident[:],
                     )
             nc.scalar.copy(
-                out=grouped_words[:, c * BANK : (c + 1) * BANK].rearrange(
-                    "q (a r u) -> q a r u", a=2, u=2
+                out=grouped_words[:, 2 * first * P : 2 * (first + count) * P].rearrange(
+                    "q (a r u) -> q a r u", a=count, u=2
                 ),
-                in_=flipped[:].rearrange("q (a u r) -> q a r u", a=2, u=2),
+                in_=flipped[:].rearrange("q (a u r) -> q a r u", a=count, u=2),
             )
 
-        def quantise(c):
-            cols = slice(2 * c * P, (2 * c + 2) * P)
+        def quantise(first, count):
+            cols = slice(first * P, (first + count) * P)
             nc.vector.quantize_mx(
                 out=codes[:, cols].bitcast(FP8X4),
                 scales=planes[:, cols],
-                in_=grouped[:, 8 * c * P : 8 * (c + 1) * P],
+                in_=grouped[:, 4 * first * P : 4 * (first + count) * P],
             )
 
         def spread_bias():
@@ -233,17 +233,16 @@ def tile_dispatcher_pa_s_kernel(tc, inv, Wk_words, Wk_scales, bk, out):
         def pairs_at(s):
             return [s] if 0 <= s < PAIRS else []
 
-        flip(0)
-        quantise(0)
-        flip(1)
-        quantise(1)
+        flip(0, 1)
+        quantise(0, 1)
+        flip(1, 1)
+        quantise(1, 1)
+        flip(2, 2)
         spread_bias()
         product(0)
         for s in range(PAIRS + SUM_LAG):
             for c in pairs_at(s + FLIP_LEAD):
-                flip(c)
-            for c in pairs_at(s + PRODUCT_LEAD):
-                product(c)
+                flip(2 * c, 2)
             if s == PAIRS - 1:
                 nc.tensor.matmul(
                     out=c_next[:], lhsT=shift_up[:], rhs=c_even[:, 0, :], start=True, stop=True
@@ -254,6 +253,9 @@ def tile_dispatcher_pa_s_kernel(tc, inv, Wk_words, Wk_scales, bk, out):
                 row_gain(c)
             for c in pairs_at(s):
                 add_bias(2 * c)
+            for c in pairs_at(s + PRODUCT_LEAD):
+                quantise(2 * c, 2)
+                product(c)
             for c in pairs_at(s - CLAMP_LAG):
                 clamp(c)
             for c in pairs_at(s):
@@ -263,8 +265,6 @@ def tile_dispatcher_pa_s_kernel(tc, inv, Wk_words, Wk_scales, bk, out):
                 scale_even(c)
             for c in pairs_at(s - DIFF_LAG):
                 differences(c)
-            for c in pairs_at(s + FLIP_LEAD):
-                quantise(c)
 
         diff_col = keep.tile([P, BLOCKS], F32)
         nc.vector.tensor_reduce(out=diff_col[:], in_=partial[:], axis=AXIS.X, op=ALU.add)
@@ -282,5 +282,7 @@ def tile_dispatcher_pa_s_kernel(tc, inv, Wk_words, Wk_scales, bk, out):
                 nc.vector.tensor_copy(out=out_sb[:, 0 : D // 2], in_=spread[:])
             else:
                 nc.scalar.copy(out=out_sb[:, D // 2 : D], in_=spread[:])
-        for e in range(D // P):
-            nc.sync.dma_start(out=out[e * P : (e + 1) * P, :], in_=out_sb[:])
+        nc.sync.dma_start(
+            out=out.rearrange("(e p) d -> p e d", p=P),
+            in_=out_sb[:].unsqueeze(1).to_broadcast([P, D // P, D]),
+        )

@@ -81,13 +81,8 @@ def tile_dispatcher_pa_s_kernel(tc, inv, Wk_words, Wk_scales, bk, out):
         eps2_shrunk = const.tile([P, 1], F32)
         nc.vector.memset(eps2_shrunk[:], SHRINK * EPS * EPS)
         shift_up = const.tile([P, P], F32)
-        nc.vector.memset(shift_up[:], 0.0)
         nc.vector.tensor_copy(out=shift_up[:, 0 : P - 1], in_=ident[:, 1:P])
-        not_last = const.tile([P, 1], F32)
-        nc.vector.tensor_scalar(
-            out=not_last[:], in0=ident[:, P - 1 : P], scalar1=-1.0, scalar2=1.0,
-            op0=ALU.mult, op1=ALU.add,
-        )
+        nc.vector.tensor_copy(out=shift_up[:, P - 1 : P], in_=ident[:, 0:1])
         warm = const.tile([P, 1], F32)
         nc.scalar.activation(out=warm[:], in_=eps2_shrunk[:], func=ACT.Abs_reciprocal_sqrt)
 
@@ -104,14 +99,12 @@ def tile_dispatcher_pa_s_kernel(tc, inv, Wk_words, Wk_scales, bk, out):
         row_sq = keep.tile([P, TILES], F32)
         sq_excess = keep.tile([P, TILES], F32)
         inv_denom = keep.tile([P, TILES], F32)
-        gain = keep.tile([P, TILES + 1], F32)
-        c_even = keep.tile([P, PAIRS, D], F32)
-        delta = keep.tile([P, TILES, D], F32)
+        gain = keep.tile([P, TILES], F32)
+        signed_c = keep.tile([P, TILES, D], F32)
         abs_delta = keep.tile([P, PAIRS, BLOCKS, 2 * P], F32)
         partial = keep.tile([P, BLOCKS, PAIRS], F32)
         acc = {}
         turned = {}
-        c_next = psum_hold.tile([P, D], F32, tag="hold", name="c_next")
 
         def flip(first, count):
             flipped = psum_work.tile([P, count * 2 * P], F32, tag="work", name="flipped")
@@ -190,42 +183,42 @@ def tile_dispatcher_pa_s_kernel(tc, inv, Wk_words, Wk_scales, bk, out):
                 in1=row_sum[:, two], op0=ALU.mult, op1=ALU.mult,
             )
 
-        def scale_even(c):
+        def scale(c):
             nc.vector.tensor_scalar_mul(
-                out=c_even[:, c, :], in0=z_clamped[:, 2 * c, :], scalar1=gain[:, 2 * c : 2 * c + 1]
+                out=signed_c[:, 2 * c, :], in0=z_clamped[:, 2 * c, :],
+                scalar1=gain[:, 2 * c : 2 * c + 1],
+            )
+            nc.vector.tensor_scalar(
+                out=signed_c[:, 2 * c + 1, :], in0=z_clamped[:, 2 * c + 1, :],
+                scalar1=gain[:, 2 * c + 1 : 2 * c + 2], scalar2=-1.0, op0=ALU.mult, op1=ALU.mult,
             )
 
         def differences(c):
-            t = 2 * c + 1
-            last = c == PAIRS - 1
-            if last:
-                nc.vector.tensor_mul(
-                    out=gain[:, TILES : TILES + 1], in0=gain[:, t : t + 1], in1=not_last[:]
-                )
             for half in range(2):
                 turned[c, half] = psum_work.tile([P, BANK], F32, tag="work", name="turned")
             for a in range(2):
-                to_next = last and a == 1
-                nc.vector.scalar_tensor_tensor(
-                    out=delta[:, t - 1 + a, :], in0=z_clamped[:, t, :],
-                    scalar=gain[:, TILES : TILES + 1] if to_next else gain[:, t : t + 1],
-                    in1=c_next[:] if to_next else c_even[:, c + a, :],
-                    op0=ALU.mult, op1=ALU.subtract,
-                )
+                t = 2 * c + a
                 for block in range(BLOCKS):
                     half, b = divmod(block, 2)
-                    nc.tensor.transpose(
-                        turned[c, half][:, (2 * b + a) * P : (2 * b + a + 1) * P],
-                        delta[:, t - 1 + a, block * P : (block + 1) * P],
-                        ident[:],
+                    slot = turned[c, half][:, (2 * b + a) * P : (2 * b + a + 1) * P]
+                    cols = slice(block * P, (block + 1) * P)
+                    nc.tensor.matmul(
+                        out=slot, lhsT=signed_c[:, t, cols], rhs=ident[:],
+                        is_transpose=True, start=True, stop=False,
+                    )
+                    nc.tensor.matmul(
+                        out=slot, lhsT=signed_c[:, (t + 1) % TILES, cols],
+                        rhs=shift_up[:] if t == TILES - 1 else ident[:],
+                        is_transpose=True, start=False, stop=True,
                     )
 
         def sums(c):
             for block in range(BLOCKS):
                 half, b = divmod(block, 2)
+                width = 2 * P - 1 if c == PAIRS - 1 else 2 * P
                 nc.scalar.activation(
-                    out=abs_delta[:, c, block, :],
-                    in_=turned[c, half][:, 2 * b * P : 2 * (b + 1) * P],
+                    out=abs_delta[:, c, block, 0:width],
+                    in_=turned[c, half][:, 2 * b * P : 2 * b * P + width],
                     func=ACT.Abs,
                     accum_out=partial[:, block, c : c + 1],
                 )
@@ -243,10 +236,6 @@ def tile_dispatcher_pa_s_kernel(tc, inv, Wk_words, Wk_scales, bk, out):
         for s in range(PAIRS + SUM_LAG):
             for c in pairs_at(s + FLIP_LEAD):
                 flip(2 * c, 2)
-            if s == PAIRS - 1:
-                nc.tensor.matmul(
-                    out=c_next[:], lhsT=shift_up[:], rhs=c_even[:, 0, :], start=True, stop=True
-                )
             for c in pairs_at(s - SUM_LAG):
                 sums(c)
             for c in pairs_at(s - GAIN_LAG):
@@ -262,7 +251,7 @@ def tile_dispatcher_pa_s_kernel(tc, inv, Wk_words, Wk_scales, bk, out):
                 add_bias(2 * c + 1)
                 inverse_norm(c)
             for c in pairs_at(s - GAIN_LAG):
-                scale_even(c)
+                scale(c)
             for c in pairs_at(s - DIFF_LAG):
                 differences(c)
 

@@ -41,8 +41,8 @@ def tile_dispatcher_pa_s_kernel(tc, inv, Wk_words, Wk_scales, bk, out):
     with ExitStack() as stack:
         const = stack.enter_context(tc.tile_pool(name="const", bufs=1))
         keep = stack.enter_context(tc.tile_pool(name="keep", bufs=1))
-        psum_work = stack.enter_context(tc.psum_pool(name="psum_work", bufs=6))
-        psum_hold = stack.enter_context(tc.psum_pool(name="psum_hold", bufs=2))
+        psum_work = stack.enter_context(tc.psum_pool(name="psum_work", bufs=8))
+        psum_hold = psum_work
         stack.enter_context(tc.manual_schedule())
 
         rows = inv.flatten_outer_dims().rearrange("(p t) k -> p t k", t=TILES)
@@ -132,7 +132,7 @@ def tile_dispatcher_pa_s_kernel(tc, inv, Wk_words, Wk_scales, bk, out):
             )
 
         def spread_bias():
-            bias_ps = psum_hold.tile([P, D], F32, tag="hold", name="bias_ps")
+            bias_ps = psum_hold.tile([P, D], F32, tag="work", name="bias_ps")
             nc.tensor.matmul(out=bias_ps[:], lhsT=ones[:], rhs=bias_row[:], start=True, stop=True)
             nc.scalar.copy(out=bias_sb[:], in_=bias_ps[:])
 
@@ -212,8 +212,8 @@ def tile_dispatcher_pa_s_kernel(tc, inv, Wk_words, Wk_scales, bk, out):
                         is_transpose=True, start=False, stop=True,
                     )
 
-        def sums(c):
-            for block in range(BLOCKS):
+        def sums(c, blocks):
+            for block in blocks:
                 half, b = divmod(block, 2)
                 width = 2 * P - 1 if c == PAIRS - 1 else 2 * P
                 nc.scalar.activation(
@@ -221,6 +221,25 @@ def tile_dispatcher_pa_s_kernel(tc, inv, Wk_words, Wk_scales, bk, out):
                     in_=turned[c, half][:, 2 * b * P : 2 * b * P + width],
                     func=ACT.Abs,
                     accum_out=partial[:, block, c : c + 1],
+                )
+
+        spread_of = {}
+
+        def spread_sums(c, blocks):
+            if c == 0:
+                wide = psum_work.tile([P, 2 * P], F32, tag="work", name="spread")
+                spread_of[0] = wide[:, 0:P]
+                spread_of[1] = wide[:, P : 2 * P]
+                spread_of[0, 1] = wide[:]
+                for block in (2, 3):
+                    narrow = psum_work.tile([P, P], F32, tag="work", name="spread")
+                    spread_of[block] = narrow[:]
+            for block in blocks:
+                nc.tensor.matmul(
+                    out=spread_of[block],
+                    lhsT=partial[:, block, c : c + 1].to_broadcast([P, P]), rhs=ident[:],
+                    is_transpose=True, start=c == 0 and block != 1,
+                    stop=c == PAIRS - 1 and block != 0,
                 )
 
         def pairs_at(s):
@@ -236,8 +255,11 @@ def tile_dispatcher_pa_s_kernel(tc, inv, Wk_words, Wk_scales, bk, out):
         for s in range(PAIRS + SUM_LAG):
             for c in pairs_at(s + FLIP_LEAD):
                 flip(2 * c, 2)
+            for c in pairs_at(s - SUM_LAG - 1):
+                spread_sums(c, range(BLOCKS))
             for c in pairs_at(s - SUM_LAG):
-                sums(c)
+                if c < PAIRS - 1:
+                    sums(c, range(BLOCKS))
             for c in pairs_at(s - GAIN_LAG):
                 row_gain(c)
             for c in pairs_at(s):
@@ -255,23 +277,23 @@ def tile_dispatcher_pa_s_kernel(tc, inv, Wk_words, Wk_scales, bk, out):
             for c in pairs_at(s - DIFF_LAG):
                 differences(c)
 
-        diff_col = keep.tile([P, BLOCKS], F32)
-        nc.vector.tensor_reduce(out=diff_col[:], in_=partial[:], axis=AXIS.X, op=ALU.add)
         out_sb = keep.tile([P, D], F32)
-        for half in range(2):
-            spread = psum_hold.tile([P, D // 2], F32, tag="hold", name="spread")
-            for b in range(2):
-                block = 2 * half + b
-                nc.tensor.transpose(
-                    spread[:, b * P : (b + 1) * P],
-                    diff_col[:, block : block + 1].to_broadcast([P, P]),
-                    ident[:],
-                )
-            if half == 0:
-                nc.vector.tensor_copy(out=out_sb[:, 0 : D // 2], in_=spread[:])
-            else:
-                nc.scalar.copy(out=out_sb[:, D // 2 : D], in_=spread[:])
-        nc.sync.dma_start(
-            out=out.rearrange("(e p) d -> p e d", p=P),
-            in_=out_sb[:].unsqueeze(1).to_broadcast([P, D // P, D]),
-        )
+        out_rows = out.rearrange("(e p) d -> p e d", p=P)
+
+        def store(half):
+            cols = slice(half * (D // 2), (half + 1) * (D // 2))
+            nc.sync.dma_start(
+                out=out_rows[:, :, cols],
+                in_=out_sb[:, cols].unsqueeze(1).to_broadcast([P, D // P, D // 2]),
+            )
+
+        last = PAIRS - 1
+        sums(last, (0, 1))
+        spread_sums(last, (0, 1))
+        nc.vector.tensor_copy(out=out_sb[:, 0 : 2 * P], in_=spread_of[0, 1])
+        store(0)
+        sums(last, (2, 3))
+        spread_sums(last, (2, 3))
+        nc.vector.tensor_copy(out=out_sb[:, 2 * P : 3 * P], in_=spread_of[2])
+        nc.scalar.copy(out=out_sb[:, 3 * P : 4 * P], in_=spread_of[3])
+        store(1)

@@ -30,7 +30,6 @@ FLIP_LEAD = 2
 PRODUCT_LEAD = 1
 CLAMP_LAG = 1
 GAIN_LAG = 2
-DIFF_LAG = 3
 SUM_LAG = 4
 
 FLOPS = 2 * ROWS * D * D
@@ -102,7 +101,8 @@ def tile_dispatcher_pa_s_kernel(tc, inv, Wk_words, Wk_scales, bk, out):
         gain = keep.tile([P, TILES], F32)
         signed_c = keep.tile([P, TILES, D], F32)
         abs_delta = keep.tile([P, PAIRS, BLOCKS, 2 * P], F32)
-        partial = keep.tile([P, BLOCKS, PAIRS], F32)
+        partial = keep.tile([P, BLOCKS, 2 * PAIRS], F32)
+        below_zero = keep.tile([P, PAIRS, 2, 2 * P], F32)
         acc = {}
         turned = {}
 
@@ -183,34 +183,44 @@ def tile_dispatcher_pa_s_kernel(tc, inv, Wk_words, Wk_scales, bk, out):
                 in1=row_sum[:, two], op0=ALU.mult, op1=ALU.mult,
             )
 
-        def scale(c):
-            nc.vector.tensor_scalar_mul(
-                out=signed_c[:, 2 * c, :], in0=z_clamped[:, 2 * c, :],
-                scalar1=gain[:, 2 * c : 2 * c + 1],
-            )
-            nc.vector.tensor_scalar(
-                out=signed_c[:, 2 * c + 1, :], in0=z_clamped[:, 2 * c + 1, :],
-                scalar1=gain[:, 2 * c + 1 : 2 * c + 2], scalar2=-1.0, op0=ALU.mult, op1=ALU.mult,
+        def turn_into(step, block, t, moving, first, last):
+            c, a = divmod(step, 2)
+            half, b = divmod(block, 2)
+            nc.tensor.matmul(
+                out=turned[c, half][:, (2 * b + a) * P : (2 * b + a + 1) * P],
+                lhsT=signed_c[:, t, block * P : (block + 1) * P], rhs=moving,
+                is_transpose=True, start=first, stop=last,
             )
 
-        def differences(c):
+        def open_banks(c):
             for half in range(2):
                 turned[c, half] = psum_work.tile([P, BANK], F32, tag="work", name="turned")
-            for a in range(2):
-                t = 2 * c + a
-                for block in range(BLOCKS):
-                    half, b = divmod(block, 2)
-                    slot = turned[c, half][:, (2 * b + a) * P : (2 * b + a + 1) * P]
-                    cols = slice(block * P, (block + 1) * P)
-                    nc.tensor.matmul(
-                        out=slot, lhsT=signed_c[:, t, cols], rhs=ident[:],
-                        is_transpose=True, start=True, stop=False,
-                    )
-                    nc.tensor.matmul(
-                        out=slot, lhsT=signed_c[:, (t + 1) % TILES, cols],
-                        rhs=shift_up[:] if t == TILES - 1 else ident[:],
-                        is_transpose=True, start=False, stop=True,
-                    )
+
+        def turn(t):
+            if t % 2 == 0 and t < TILES - 2:
+                open_banks(t // 2)
+            for block in range(BLOCKS):
+                if t > 0:
+                    turn_into(t - 1, block, t, ident[:], False, t % 2 == 0 and block % 2 == 1)
+                turn_into(
+                    t, block, t, ident[:], t % 2 == 0 and t < TILES - 2 and block % 2 == 0,
+                    t == TILES - 1 and block % 2 == 1,
+                )
+
+        def turn_shifted():
+            open_banks(PAIRS - 1)
+            for block in range(BLOCKS):
+                turn_into(TILES - 1, block, 0, shift_up[:], block % 2 == 0, False)
+
+        def scale(c):
+            for t in (2 * c, 2 * c + 1):
+                nc.vector.tensor_scalar(
+                    out=signed_c[:, t, :], in0=z_clamped[:, t, :], scalar1=gain[:, t : t + 1],
+                    scalar2=1.0 if t % 2 == 0 else -1.0, op0=ALU.mult, op1=ALU.mult,
+                )
+                turn(t)
+            if c == 1:
+                turn_shifted()
 
         def sums(c, blocks):
             for block in blocks:
@@ -223,24 +233,35 @@ def tile_dispatcher_pa_s_kernel(tc, inv, Wk_words, Wk_scales, bk, out):
                     accum_out=partial[:, block, c : c + 1],
                 )
 
+        def vector_sums(c, positive):
+            for b in range(2):
+                block = 2 + b
+                column = c if positive else PAIRS + c
+                nc.vector.tensor_scalar(
+                    out=abs_delta[:, c, block, :] if positive else below_zero[:, c, b, :],
+                    in0=turned[c, 1][:, 2 * b * P : 2 * (b + 1) * P],
+                    scalar1=0.0, scalar2=None, op0=ALU.max if positive else ALU.min,
+                    op1=ALU.add if positive else ALU.subtract,
+                    accum_out=partial[:, block, column : column + 1],
+                )
+
         spread_of = {}
 
-        def spread_sums(c, blocks):
+        def spread(block, column, first, last):
+            nc.tensor.matmul(
+                out=spread_of[block],
+                lhsT=partial[:, block, column : column + 1].to_broadcast([P, P]), rhs=ident[:],
+                is_transpose=True, start=first, stop=last,
+            )
+
+        def spread_first_half(c):
             if c == 0:
                 wide = psum_work.tile([P, 2 * P], F32, tag="work", name="spread")
                 spread_of[0] = wide[:, 0:P]
                 spread_of[1] = wide[:, P : 2 * P]
                 spread_of[0, 1] = wide[:]
-                for block in (2, 3):
-                    narrow = psum_work.tile([P, P], F32, tag="work", name="spread")
-                    spread_of[block] = narrow[:]
-            for block in blocks:
-                nc.tensor.matmul(
-                    out=spread_of[block],
-                    lhsT=partial[:, block, c : c + 1].to_broadcast([P, P]), rhs=ident[:],
-                    is_transpose=True, start=c == 0 and block != 1,
-                    stop=c == PAIRS - 1 and block != 0,
-                )
+            spread(0, c, c == 0, False)
+            spread(1, c, False, c == PAIRS - 1)
 
         def pairs_at(s):
             return [s] if 0 <= s < PAIRS else []
@@ -256,10 +277,10 @@ def tile_dispatcher_pa_s_kernel(tc, inv, Wk_words, Wk_scales, bk, out):
             for c in pairs_at(s + FLIP_LEAD):
                 flip(2 * c, 2)
             for c in pairs_at(s - SUM_LAG - 1):
-                spread_sums(c, range(BLOCKS))
+                spread_first_half(c)
             for c in pairs_at(s - SUM_LAG):
                 if c < PAIRS - 1:
-                    sums(c, range(BLOCKS))
+                    sums(c, range(BLOCKS) if c == 0 else (0, 1))
             for c in pairs_at(s - GAIN_LAG):
                 row_gain(c)
             for c in pairs_at(s):
@@ -274,8 +295,9 @@ def tile_dispatcher_pa_s_kernel(tc, inv, Wk_words, Wk_scales, bk, out):
                 inverse_norm(c)
             for c in pairs_at(s - GAIN_LAG):
                 scale(c)
-            for c in pairs_at(s - DIFF_LAG):
-                differences(c)
+                if c == PAIRS - 1:
+                    vector_sums(1, True)
+                    vector_sums(1, False)
 
         out_sb = keep.tile([P, D], F32)
         out_rows = out.rearrange("(e p) d -> p e d", p=P)
@@ -289,11 +311,18 @@ def tile_dispatcher_pa_s_kernel(tc, inv, Wk_words, Wk_scales, bk, out):
 
         last = PAIRS - 1
         sums(last, (0, 1))
-        spread_sums(last, (0, 1))
+        spread_first_half(last)
         nc.vector.tensor_copy(out=out_sb[:, 0 : 2 * P], in_=spread_of[0, 1])
         store(0)
+        sums(2, (2, 3))
         sums(last, (2, 3))
-        spread_sums(last, (2, 3))
+        columns = (0, 1, PAIRS + 1, 2, last)
+        for block in (2, 3):
+            narrow = psum_work.tile([P, P], F32, tag="work", name="spread")
+            spread_of[block] = narrow[:]
+        for column in columns:
+            for block in (2, 3):
+                spread(block, column, column == columns[0], column == columns[-1])
         nc.vector.tensor_copy(out=out_sb[:, 2 * P : 3 * P], in_=spread_of[2])
         nc.scalar.copy(out=out_sb[:, 3 * P : 4 * P], in_=spread_of[3])
         store(1)

@@ -44,6 +44,14 @@ def tile_dispatcher_pa_s_kernel(tc, inv, Wk_words, Wk_scales, bk, out):
         psum_hold = psum_work
         stack.enter_context(tc.manual_schedule())
 
+        idle_sb = const.tile([P, D], BF16)
+        nc.vector.memset(idle_sb[:], 1.0)
+        idle_ps = psum_work.tile([P, D], F32, tag="work", name="idle_ps")
+        for again in range(2):
+            nc.tensor.matmul(
+                out=idle_ps[:], lhsT=idle_sb[:, 0:P], rhs=idle_sb[:], start=True, stop=True
+            )
+
         rows = inv.flatten_outer_dims().rearrange("(p t) k -> p t k", t=TILES)
         x_sb = keep.tile([P, TILES, D], BF16)
 
@@ -134,7 +142,7 @@ def tile_dispatcher_pa_s_kernel(tc, inv, Wk_words, Wk_scales, bk, out):
         def spread_bias():
             bias_ps = psum_hold.tile([P, D], F32, tag="work", name="bias_ps")
             nc.tensor.matmul(out=bias_ps[:], lhsT=ones[:], rhs=bias_row[:], start=True, stop=True)
-            nc.scalar.copy(out=bias_sb[:], in_=bias_ps[:])
+            nc.vector.tensor_copy(out=bias_sb[:], in_=bias_ps[:])
 
         def product(c):
             for t in (2 * c, 2 * c + 1):
@@ -270,8 +278,8 @@ def tile_dispatcher_pa_s_kernel(tc, inv, Wk_words, Wk_scales, bk, out):
         quantise(0, 1)
         flip(1, 1)
         quantise(1, 1)
-        flip(2, 2)
         spread_bias()
+        flip(2, 2)
         product(0)
         for s in range(PAIRS + SUM_LAG):
             for c in pairs_at(s + FLIP_LEAD):

@@ -44,14 +44,6 @@ def tile_dispatcher_pa_s_kernel(tc, inv, Wk_words, Wk_scales, bk, out):
         psum_hold = psum_work
         stack.enter_context(tc.manual_schedule())
 
-        idle_sb = const.tile([P, D], BF16)
-        nc.vector.memset(idle_sb[:], 1.0)
-        idle_ps = psum_work.tile([P, D], F32, tag="work", name="idle_ps")
-        for again in range(2):
-            nc.tensor.matmul(
-                out=idle_ps[:], lhsT=idle_sb[:, 0:P], rhs=idle_sb[:], start=True, stop=True
-            )
-
         rows = inv.flatten_outer_dims().rearrange("(p t) k -> p t k", t=TILES)
         x_sb = keep.tile([P, TILES, D], BF16)
 
@@ -59,7 +51,7 @@ def tile_dispatcher_pa_s_kernel(tc, inv, Wk_words, Wk_scales, bk, out):
             nc.sync.dma_start(out=x_sb[:, 2 * c : 2 * c + 2, :], in_=rows[:, 2 * c : 2 * c + 2, :])
 
         bias_row = const.tile([P, D], BF16)
-        nc.gpsimd.memset(bias_row[:], 0.0)
+        nc.gpsimd.memset(bias_row[:].bitcast(F32), 0.0)
         nc.scalar.dma_start(out=bias_row[0:1, :], in_=bk.rearrange("(o n) -> o n", o=1))
         load_pair(0)
         load_pair(1)
@@ -79,19 +71,27 @@ def tile_dispatcher_pa_s_kernel(tc, inv, Wk_words, Wk_scales, bk, out):
         load_pair(2)
         load_pair(3)
 
-        ident = const.tile([P, P], F32)
-        make_identity(nc, ident[:])
-        ones = const.tile([P, P], BF16)
-        nc.gpsimd.memset(ones[:], 1.0)
         minus_eps2 = const.tile([P, 1], F32)
         nc.vector.memset(minus_eps2[:], -EPS * EPS)
         eps2_shrunk = const.tile([P, 1], F32)
         nc.vector.memset(eps2_shrunk[:], SHRINK * EPS * EPS)
+        warm = const.tile([P, 1], F32)
+        nc.scalar.activation(out=warm[:], in_=eps2_shrunk[:], func=ACT.Abs_reciprocal_sqrt)
+        idle_sb = const.tile([P, D], BF16)
+        nc.vector.memset(idle_sb[:], 1.0)
+        idle_ps = psum_work.tile([P, D], F32, tag="work", name="idle_ps")
+        for again in range(2):
+            nc.tensor.matmul(
+                out=idle_ps[:], lhsT=idle_sb[:, 0:P], rhs=idle_sb[:], start=True, stop=True
+            )
+
+        ident = const.tile([P, P], F32)
+        make_identity(nc, ident[:])
+        ones = const.tile([P, P], BF16)
+        nc.gpsimd.memset(ones[:], 1.0)
         shift_up = const.tile([P, P], F32)
         nc.vector.tensor_copy(out=shift_up[:, 0 : P - 1], in_=ident[:, 1:P])
         nc.vector.tensor_copy(out=shift_up[:, P - 1 : P], in_=ident[:, 0:1])
-        warm = const.tile([P, 1], F32)
-        nc.scalar.activation(out=warm[:], in_=eps2_shrunk[:], func=ACT.Abs_reciprocal_sqrt)
 
         x_words = x_sb[:].rearrange("p t k -> p (t k)").bitcast(F32)
         grouped = keep.tile([P, TILES * P * 4], BF16, align_bytes=64)

@@ -28,9 +28,7 @@ SHRINK = 2.0 ** -32
 
 FLIP_LEAD = 2
 PRODUCT_LEAD = 1
-CLAMP_LAG = 1
-GAIN_LAG = 2
-SUM_LAG = 4
+GAIN_LAG = 1
 
 FLOPS = 2 * ROWS * D * D
 
@@ -40,8 +38,11 @@ def tile_dispatcher_pa_s_kernel(tc, inv, Wk_words, Wk_scales, bk, out):
     with ExitStack() as stack:
         const = stack.enter_context(tc.tile_pool(name="const", bufs=1))
         keep = stack.enter_context(tc.tile_pool(name="keep", bufs=1))
-        psum_work = stack.enter_context(tc.psum_pool(name="psum_work", bufs=8))
-        psum_hold = psum_work
+        psum = stack.enter_context(tc.psum_pool(name="psum", bufs=1))
+
+        def bank(number, width, name):
+            return psum.tile([P, width], F32, tag="bank%d" % number, name=name)
+
         stack.enter_context(tc.manual_schedule())
 
         rows = inv.flatten_outer_dims().rearrange("(p t) k -> p t k", t=TILES)
@@ -79,14 +80,22 @@ def tile_dispatcher_pa_s_kernel(tc, inv, Wk_words, Wk_scales, bk, out):
         nc.scalar.activation(out=warm[:], in_=eps2_shrunk[:], func=ACT.Abs_reciprocal_sqrt)
         idle_sb = const.tile([P, D], BF16)
         nc.vector.memset(idle_sb[:], 1.0)
-        idle_ps = psum_work.tile([P, D], F32, tag="work", name="idle_ps")
-        for again in range(2):
+        idle_ps = bank(5, D, "idle_ps")
+        for width in (D, D // 2):
             nc.tensor.matmul(
-                out=idle_ps[:], lhsT=idle_sb[:, 0:P], rhs=idle_sb[:], start=True, stop=True
+                out=idle_ps[:, 0:width], lhsT=idle_sb[:, 0:P], rhs=idle_sb[:, 0:width],
+                start=True, stop=True,
             )
 
         ident = const.tile([P, P], F32)
         make_identity(nc, ident[:])
+        ends = const.tile([P, 2], F32)
+        nc.vector.tensor_scalar(
+            out=ends[:, 0:1], in0=ident[:, 0:1], scalar1=-0.5, scalar2=None, op0=ALU.mult
+        )
+        nc.vector.tensor_scalar(
+            out=ends[:, 1:2], in0=ident[:, P - 1 : P], scalar1=-0.5, scalar2=None, op0=ALU.mult
+        )
         ones = const.tile([P, P], BF16)
         nc.gpsimd.memset(ones[:], 1.0)
         shift_up = const.tile([P, P], F32)
@@ -108,14 +117,13 @@ def tile_dispatcher_pa_s_kernel(tc, inv, Wk_words, Wk_scales, bk, out):
         inv_denom = keep.tile([P, TILES], F32)
         gain = keep.tile([P, TILES], F32)
         signed_c = keep.tile([P, TILES, D], F32)
-        abs_delta = keep.tile([P, PAIRS, BLOCKS, 2 * P], F32)
-        partial = keep.tile([P, BLOCKS, 2 * PAIRS], F32)
-        below_zero = keep.tile([P, PAIRS, 2, 2 * P], F32)
+        written = keep.tile([P, 10, BANK], F32)
+        partial = keep.tile([P, BLOCKS, 3], F32)
         acc = {}
         turned = {}
 
         def flip(first, count):
-            flipped = psum_work.tile([P, count * 2 * P], F32, tag="work", name="flipped")
+            flipped = bank((first + 1) // 2 if first > 1 else first + 5, count * 2 * P, "flipped")
             for a in range(count):
                 t = first + a
                 for u in range(2):
@@ -140,13 +148,13 @@ def tile_dispatcher_pa_s_kernel(tc, inv, Wk_words, Wk_scales, bk, out):
             )
 
         def spread_bias():
-            bias_ps = psum_hold.tile([P, D], F32, tag="work", name="bias_ps")
+            bias_ps = bank(4, D, "bias_ps")
             nc.tensor.matmul(out=bias_ps[:], lhsT=ones[:], rhs=bias_row[:], start=True, stop=True)
             nc.vector.tensor_copy(out=bias_sb[:], in_=bias_ps[:])
 
         def product(c):
             for t in (2 * c, 2 * c + 1):
-                acc[t] = psum_work.tile([P, BANK], F32, tag="work", name="acc")
+                acc[t] = bank((0, 6, 5, 7, 5, 6, 7, 5)[t], BANK, "acc")
                 nc.tensor.matmul_mx(
                     out=acc[t][:],
                     lhsT=codes[:, t * P : (t + 1) * P].bitcast(FP8X4),
@@ -162,6 +170,8 @@ def tile_dispatcher_pa_s_kernel(tc, inv, Wk_words, Wk_scales, bk, out):
                 out=z[:, t, :], in0=acc[t][:], scalar=1.0, in1=bias_sb[:],
                 op0=ALU.mult, op1=ALU.add, accum_out=row_sum[:, t : t + 1],
             )
+
+        def square(t):
             nc.scalar.activation(
                 out=squares[:, t, :], in_=z[:, t, :], func=ACT.Square,
                 accum_out=row_sq[:, t : t + 1],
@@ -178,11 +188,11 @@ def tile_dispatcher_pa_s_kernel(tc, inv, Wk_words, Wk_scales, bk, out):
             )
 
         def clamp(c):
-            two = slice(2 * c, 2 * c + 2)
-            nc.vector.tensor_scalar(
-                out=z_clamped[:, two, :], in0=z[:, two, :], scalar1=CLAMP, scalar2=-CLAMP,
-                op0=ALU.min, op1=ALU.max,
-            )
+            for t in (2 * c, 2 * c + 1):
+                nc.vector.tensor_scalar(
+                    out=z_clamped[:, t, :], in0=z[:, t, :], scalar1=CLAMP, scalar2=-CLAMP,
+                    op0=ALU.min, op1=ALU.max,
+                )
 
         def row_gain(c):
             two = slice(2 * c, 2 * c + 2)
@@ -191,67 +201,68 @@ def tile_dispatcher_pa_s_kernel(tc, inv, Wk_words, Wk_scales, bk, out):
                 in1=row_sum[:, two], op0=ALU.mult, op1=ALU.mult,
             )
 
-        def turn_into(step, block, t, moving, first, last):
-            c, a = divmod(step, 2)
-            half, b = divmod(block, 2)
-            nc.tensor.matmul(
-                out=turned[c, half][:, (2 * b + a) * P : (2 * b + a + 1) * P],
-                lhsT=signed_c[:, t, block * P : (block + 1) * P], rhs=moving,
-                is_transpose=True, start=first, stop=last,
+        def scale(t):
+            nc.vector.tensor_scalar(
+                out=signed_c[:, t, :], in0=z_clamped[:, t, :], scalar1=gain[:, t : t + 1],
+                scalar2=2.0 if t % 2 == 0 else -2.0, op0=ALU.mult, op1=ALU.mult,
             )
 
-        def open_banks(c):
-            for half in range(2):
-                turned[c, half] = psum_work.tile([P, BANK], F32, tag="work", name="turned")
+        LAST_BLOCK = BLOCKS - 1
+
+        def place(step, block):
+            if block == LAST_BLOCK:
+                return (block, step % 2), step // 2
+            return (block, step // 4), step % 4
+
+        bank_of = {}
+        for block in range(LAST_BLOCK):
+            bank_of[block, 0] = 1 + block
+            bank_of[block, 1] = 5 + block
+        bank_of[LAST_BLOCK, 0] = 4
+        bank_of[LAST_BLOCK, 1] = 0
+        count_left = {}
+
+        def turn_into(step, block, t, moving):
+            key, column = place(step, block)
+            first = key not in turned
+            if first:
+                turned[key] = bank(bank_of[key], BANK, "turned")
+                count_left[key] = 8
+            count_left[key] -= 1
+            nc.tensor.matmul(
+                out=turned[key][:, column * P : (column + 1) * P],
+                lhsT=signed_c[:, t, block * P : (block + 1) * P], rhs=moving,
+                is_transpose=True, start=first, stop=count_left[key] == 0,
+            )
 
         def turn(t):
-            if t % 2 == 0 and t < TILES - 2:
-                open_banks(t // 2)
             for block in range(BLOCKS):
-                if t > 0:
-                    turn_into(t - 1, block, t, ident[:], False, t % 2 == 0 and block % 2 == 1)
-                turn_into(
-                    t, block, t, ident[:], t % 2 == 0 and t < TILES - 2 and block % 2 == 0,
-                    t == TILES - 1 and block % 2 == 1,
-                )
+                turn_block(t, block)
+
+        def turn_block(t, block):
+            if t > 0:
+                turn_into(t - 1, block, t, ident[:])
+            turn_into(t, block, t, ident[:])
 
         def turn_shifted():
-            open_banks(PAIRS - 1)
             for block in range(BLOCKS):
-                turn_into(TILES - 1, block, 0, shift_up[:], block % 2 == 0, False)
+                turn_into(TILES - 1, block, 0, shift_up[:])
 
-        def scale(c):
-            for t in (2 * c, 2 * c + 1):
-                nc.vector.tensor_scalar(
-                    out=signed_c[:, t, :], in0=z_clamped[:, t, :], scalar1=gain[:, t : t + 1],
-                    scalar2=1.0 if t % 2 == 0 else -1.0, op0=ALU.mult, op1=ALU.mult,
-                )
-                turn(t)
-            if c == 1:
-                turn_shifted()
+        def scalar_sum(block, late):
+            width = BANK - 1 if late else BANK
+            nc.scalar.activation(
+                out=written[:, 2 * block + late, 0:width], in_=turned[block, late][:, 0:width],
+                func=ACT.Abs, scale=1.0 if block == 2 else 0.5,
+                accum_out=partial[:, block, (2 if block == 2 else late) : (2 if block == 2 else late) + 1],
+            )
 
-        def sums(c, blocks):
-            for block in blocks:
-                half, b = divmod(block, 2)
-                width = 2 * P - 1 if c == PAIRS - 1 else 2 * P
-                nc.scalar.activation(
-                    out=abs_delta[:, c, block, 0:width],
-                    in_=turned[c, half][:, 2 * b * P : 2 * b * P + width],
-                    func=ACT.Abs,
-                    accum_out=partial[:, block, c : c + 1],
-                )
-
-        def vector_sums(c, positive):
-            for b in range(2):
-                block = 2 + b
-                column = c if positive else PAIRS + c
-                nc.vector.tensor_scalar(
-                    out=abs_delta[:, c, block, :] if positive else below_zero[:, c, b, :],
-                    in0=turned[c, 1][:, 2 * b * P : 2 * (b + 1) * P],
-                    scalar1=0.0, scalar2=None, op0=ALU.max if positive else ALU.min,
-                    op1=ALU.add if positive else ALU.subtract,
-                    accum_out=partial[:, block, column : column + 1],
-                )
+        def vector_sum(key, width, positive, slot, block, which):
+            nc.vector.tensor_scalar(
+                out=written[:, slot, 0:width], in0=turned[key][:, 0:width],
+                scalar1=0.0, scalar2=None, op0=ALU.max if positive else ALU.min,
+                op1=ALU.add if positive else ALU.subtract,
+                accum_out=partial[:, block, which : which + 1],
+            )
 
         spread_of = {}
 
@@ -262,50 +273,58 @@ def tile_dispatcher_pa_s_kernel(tc, inv, Wk_words, Wk_scales, bk, out):
                 is_transpose=True, start=first, stop=last,
             )
 
-        def spread_first_half(c):
-            if c == 0:
-                wide = psum_work.tile([P, 2 * P], F32, tag="work", name="spread")
-                spread_of[0] = wide[:, 0:P]
-                spread_of[1] = wide[:, P : 2 * P]
-                spread_of[0, 1] = wide[:]
-            spread(0, c, c == 0, False)
-            spread(1, c, False, c == PAIRS - 1)
+        def add_end(which, first):
+            t = which * (TILES - 1)
+            nc.tensor.matmul(
+                out=spread_of[LAST_BLOCK], lhsT=ends[:, which : which + 1].to_broadcast([P, P]),
+                rhs=signed_c[:, t, LAST_BLOCK * P :], start=first, stop=False,
+            )
 
         def pairs_at(s):
             return [s] if 0 <= s < PAIRS else []
 
+        last = PAIRS - 1
+        spread_bias()
         flip(0, 1)
         quantise(0, 1)
         flip(1, 1)
         quantise(1, 1)
-        spread_bias()
         flip(2, 2)
         product(0)
-        for s in range(PAIRS + SUM_LAG):
+        for s in range(PAIRS):
+            add_bias(2 * s)
             for c in pairs_at(s + FLIP_LEAD):
                 flip(2 * c, 2)
-            for c in pairs_at(s - SUM_LAG - 1):
-                spread_first_half(c)
-            for c in pairs_at(s - SUM_LAG):
-                if c < PAIRS - 1:
-                    sums(c, range(BLOCKS) if c == 0 else (0, 1))
-            for c in pairs_at(s - GAIN_LAG):
-                row_gain(c)
-            for c in pairs_at(s):
-                add_bias(2 * c)
+            square(2 * s)
             for c in pairs_at(s + PRODUCT_LEAD):
                 quantise(2 * c, 2)
                 product(c)
-            for c in pairs_at(s - CLAMP_LAG):
-                clamp(c)
-            for c in pairs_at(s):
-                add_bias(2 * c + 1)
-                inverse_norm(c)
+            add_bias(2 * s + 1)
+            square(2 * s + 1)
+            inverse_norm(s)
             for c in pairs_at(s - GAIN_LAG):
-                scale(c)
-                if c == PAIRS - 1:
-                    vector_sums(1, True)
-                    vector_sums(1, False)
+                row_gain(c)
+                clamp(c)
+                if c == last - 1:
+                    turn_shifted()
+                for t in (2 * c, 2 * c + 1):
+                    scale(t)
+                    turn(t)
+        clamp(last)
+        row_gain(last)
+        for t in (TILES - 2, TILES - 1):
+            scale(t)
+        for block in (0, 3, 1, 2):
+            for t in (TILES - 2, TILES - 1):
+                turn_block(t, block)
+        scalar_sum(0, 0)
+        scalar_sum(1, 0)
+        vector_sum((2, 0), BANK, True, 6, 2, 0)
+        vector_sum((2, 0), BANK, False, 7, 2, 1)
+        scalar_sum(0, 1)
+        scalar_sum(1, 1)
+        vector_sum((LAST_BLOCK, 0), BANK, True, 8, LAST_BLOCK, 0)
+        vector_sum((LAST_BLOCK, 1), BANK - 1, False, 9, LAST_BLOCK, 1)
 
         out_sb = keep.tile([P, D], F32)
         out_rows = out.rearrange("(e p) d -> p e d", p=P)
@@ -317,20 +336,29 @@ def tile_dispatcher_pa_s_kernel(tc, inv, Wk_words, Wk_scales, bk, out):
                 in_=out_sb[:, cols].unsqueeze(1).to_broadcast([P, D // P, D // 2]),
             )
 
-        last = PAIRS - 1
-        sums(last, (0, 1))
-        spread_first_half(last)
-        nc.vector.tensor_copy(out=out_sb[:, 0 : 2 * P], in_=spread_of[0, 1])
+        narrow = bank(2, P, "spread")
+        spread_of[3] = narrow[:]
+        add_end(0, True)
+        add_end(1, False)
+        wide = bank(1, 2 * P, "spread")
+        spread_of[0] = wide[:, 0:P]
+        spread_of[1] = wide[:, P : 2 * P]
+        spread(0, 0, True, False)
+        spread(1, 0, False, False)
+        spread(0, 1, False, False)
+        spread(1, 1, False, True)
+        nc.vector.tensor_copy(out=out_sb[:, 0 : 2 * P], in_=wide[:])
         store(0)
-        sums(2, (2, 3))
-        sums(last, (2, 3))
-        columns = (0, 1, PAIRS + 1, 2, last)
-        for block in (2, 3):
-            narrow = psum_work.tile([P, P], F32, tag="work", name="spread")
-            spread_of[block] = narrow[:]
-        for column in columns:
-            for block in (2, 3):
-                spread(block, column, column == columns[0], column == columns[-1])
-        nc.vector.tensor_copy(out=out_sb[:, 2 * P : 3 * P], in_=spread_of[2])
-        nc.scalar.copy(out=out_sb[:, 3 * P : 4 * P], in_=spread_of[3])
+        scalar_sum(2, 1)
+        narrow = bank(3, P, "spread")
+        spread_of[2] = narrow[:]
+        spread(2, 0, True, False)
+        spread(2, 1, False, False)
+        spread(3, 0, False, False)
+        spread(3, 1, False, True)
+        spread(2, 2, False, True)
+        nc.vector.tensor_copy(out=out_sb[:, 3 * P : 4 * P], in_=spread_of[3])
+        nc.scalar.activation(
+            out=out_sb[:, 2 * P : 3 * P], in_=spread_of[2], func=ACT.Copy, scale=0.5
+        )
         store(1)

@@ -117,8 +117,8 @@ def tile_dispatcher_pa_s_kernel(tc, inv, Wk_words, Wk_scales, bk, out):
         inv_denom = keep.tile([P, TILES], F32)
         gain = keep.tile([P, TILES], F32)
         signed_c = keep.tile([P, TILES, D], F32)
-        written = keep.tile([P, 10, BANK], F32)
-        partial = keep.tile([P, BLOCKS, 3], F32)
+        written = keep.tile([P, TILES, BANK], F32)
+        partial = keep.tile([P, BLOCKS, 2], F32)
         acc = {}
         turned = {}
 
@@ -197,14 +197,20 @@ def tile_dispatcher_pa_s_kernel(tc, inv, Wk_words, Wk_scales, bk, out):
         def row_gain(c):
             two = slice(2 * c, 2 * c + 2)
             nc.vector.scalar_tensor_tensor(
-                out=gain[:, two], in0=inv_denom[:, two], scalar=math.sqrt(SHRINK) / EPS,
+                out=gain[:, two], in0=inv_denom[:, two], scalar=-2.0 * math.sqrt(SHRINK) / EPS,
                 in1=row_sum[:, two], op0=ALU.mult, op1=ALU.mult,
+            )
+
+        def scale_on_scalar(t):
+            nc.scalar.activation(
+                out=signed_c[:, t, :], in_=z_clamped[:, t, :], func=ACT.Copy,
+                scale=gain[:, t : t + 1],
             )
 
         def scale(t):
             nc.vector.tensor_scalar(
                 out=signed_c[:, t, :], in0=z_clamped[:, t, :], scalar1=gain[:, t : t + 1],
-                scalar2=2.0 if t % 2 == 0 else -2.0, op0=ALU.mult, op1=ALU.mult,
+                scalar2=-1.0 if t % 2 == 0 else 1.0, op0=ALU.mult, op1=ALU.mult,
             )
 
         LAST_BLOCK = BLOCKS - 1
@@ -252,8 +258,8 @@ def tile_dispatcher_pa_s_kernel(tc, inv, Wk_words, Wk_scales, bk, out):
             width = BANK - 1 if late else BANK
             nc.scalar.activation(
                 out=written[:, 2 * block + late, 0:width], in_=turned[block, late][:, 0:width],
-                func=ACT.Abs, scale=1.0 if block == 2 else 0.5,
-                accum_out=partial[:, block, (2 if block == 2 else late) : (2 if block == 2 else late) + 1],
+                func=ACT.Abs, scale=0.5,
+                accum_out=partial[:, block, late : late + 1],
             )
 
         def vector_sum(key, width, positive, slot, block, which):
@@ -284,47 +290,57 @@ def tile_dispatcher_pa_s_kernel(tc, inv, Wk_words, Wk_scales, bk, out):
             return [s] if 0 <= s < PAIRS else []
 
         last = PAIRS - 1
-        spread_bias()
         flip(0, 1)
         quantise(0, 1)
         flip(1, 1)
         quantise(1, 1)
+        spread_bias()
         flip(2, 2)
         product(0)
+        waiting = []
         for s in range(PAIRS):
-            add_bias(2 * s)
             for c in pairs_at(s + FLIP_LEAD):
                 flip(2 * c, 2)
+            add_bias(2 * s)
+            if s == 0:
+                quantise(2, 2)
+                product(1)
             square(2 * s)
-            for c in pairs_at(s + PRODUCT_LEAD):
-                quantise(2 * c, 2)
-                product(c)
+            if 0 < s < PAIRS - 1:
+                quantise(2 * s + 2, 2)
+                product(s + 1)
+            for t in waiting:
+                turn(t)
+            waiting.clear()
             add_bias(2 * s + 1)
             square(2 * s + 1)
-            inverse_norm(s)
             for c in pairs_at(s - GAIN_LAG):
                 row_gain(c)
                 clamp(c)
                 if c == last - 1:
                     turn_shifted()
                 for t in (2 * c, 2 * c + 1):
-                    scale(t)
-                    turn(t)
+                    if t in (1, 3):
+                        scale_on_scalar(t)
+                        waiting.append(t)
+                    else:
+                        scale(t)
+                        turn(t)
+            inverse_norm(s)
         clamp(last)
         row_gain(last)
         for t in (TILES - 2, TILES - 1):
             scale(t)
-        for block in (0, 3, 1, 2):
+        for block in (0, 1, 3, 2):
             for t in (TILES - 2, TILES - 1):
                 turn_block(t, block)
         scalar_sum(0, 0)
         scalar_sum(1, 0)
-        vector_sum((2, 0), BANK, True, 6, 2, 0)
-        vector_sum((2, 0), BANK, False, 7, 2, 1)
+        scalar_sum(2, 0)
         scalar_sum(0, 1)
         scalar_sum(1, 1)
-        vector_sum((LAST_BLOCK, 0), BANK, True, 8, LAST_BLOCK, 0)
-        vector_sum((LAST_BLOCK, 1), BANK - 1, False, 9, LAST_BLOCK, 1)
+        vector_sum((LAST_BLOCK, 0), BANK, True, 6, LAST_BLOCK, 0)
+        vector_sum((LAST_BLOCK, 1), BANK - 1, False, 7, LAST_BLOCK, 1)
 
         out_sb = keep.tile([P, D], F32)
         out_rows = out.rearrange("(e p) d -> p e d", p=P)
@@ -336,10 +352,6 @@ def tile_dispatcher_pa_s_kernel(tc, inv, Wk_words, Wk_scales, bk, out):
                 in_=out_sb[:, cols].unsqueeze(1).to_broadcast([P, D // P, D // 2]),
             )
 
-        narrow = bank(2, P, "spread")
-        spread_of[3] = narrow[:]
-        add_end(0, True)
-        add_end(1, False)
         wide = bank(1, 2 * P, "spread")
         spread_of[0] = wide[:, 0:P]
         spread_of[1] = wide[:, P : 2 * P]
@@ -350,15 +362,16 @@ def tile_dispatcher_pa_s_kernel(tc, inv, Wk_words, Wk_scales, bk, out):
         nc.vector.tensor_copy(out=out_sb[:, 0 : 2 * P], in_=wide[:])
         store(0)
         scalar_sum(2, 1)
+        narrow = bank(2, P, "spread")
+        spread_of[3] = narrow[:]
+        add_end(0, True)
+        add_end(1, False)
         narrow = bank(3, P, "spread")
         spread_of[2] = narrow[:]
         spread(2, 0, True, False)
-        spread(2, 1, False, False)
         spread(3, 0, False, False)
         spread(3, 1, False, True)
-        spread(2, 2, False, True)
+        spread(2, 1, False, True)
         nc.vector.tensor_copy(out=out_sb[:, 3 * P : 4 * P], in_=spread_of[3])
-        nc.scalar.activation(
-            out=out_sb[:, 2 * P : 3 * P], in_=spread_of[2], func=ACT.Copy, scale=0.5
-        )
+        nc.scalar.copy(out=out_sb[:, 2 * P : 3 * P], in_=spread_of[2])
         store(1)

@@ -24,7 +24,9 @@ PAIRS = TILES // 2
 BLOCKS = D // P
 BANK = 512
 CLAMP = EPS / math.sqrt(D)
-SHRINK = 2.0 ** -32
+SHRINK = 2.0 ** -16
+FLOOR = 2.0 ** -86
+UNIT = 2.0 * math.sqrt(SHRINK) / EPS
 
 FLIP_LEAD = 2
 PRODUCT_LEAD = 1
@@ -72,12 +74,10 @@ def tile_dispatcher_pa_s_kernel(tc, inv, Wk_words, Wk_scales, bk, out):
         load_pair(2)
         load_pair(3)
 
-        minus_eps2 = const.tile([P, 1], F32)
-        nc.vector.memset(minus_eps2[:], -EPS * EPS)
-        eps2_shrunk = const.tile([P, 1], F32)
-        nc.vector.memset(eps2_shrunk[:], SHRINK * EPS * EPS)
+        floor = const.tile([P, 1], F32)
+        nc.vector.memset(floor[:], FLOOR)
         warm = const.tile([P, 1], F32)
-        nc.scalar.activation(out=warm[:], in_=eps2_shrunk[:], func=ACT.Abs_reciprocal_sqrt)
+        nc.scalar.activation(out=warm[:], in_=floor[:], func=ACT.Abs_reciprocal_sqrt)
         idle_sb = const.tile([P, D], BF16)
         nc.vector.memset(idle_sb[:], 1.0)
         idle_ps = bank(5, D, "idle_ps")
@@ -113,8 +113,7 @@ def tile_dispatcher_pa_s_kernel(tc, inv, Wk_words, Wk_scales, bk, out):
         squares = keep.tile([P, TILES, D], F32)
         row_sum = keep.tile([P, TILES], F32)
         row_sq = keep.tile([P, TILES], F32)
-        sq_excess = keep.tile([P, TILES], F32)
-        inv_denom = keep.tile([P, TILES], F32)
+        inv_norm = keep.tile([P, TILES], F32)
         gain = keep.tile([P, TILES], F32)
         signed_c = keep.tile([P, TILES, D], F32)
         written = keep.tile([P, TILES, BANK], F32)
@@ -180,11 +179,8 @@ def tile_dispatcher_pa_s_kernel(tc, inv, Wk_words, Wk_scales, bk, out):
         def inverse_norm(c):
             two = slice(2 * c, 2 * c + 2)
             nc.scalar.activation(
-                out=sq_excess[:, two], in_=row_sq[:, two], func=ACT.Relu, bias=minus_eps2[:]
-            )
-            nc.scalar.activation(
-                out=inv_denom[:, two], in_=sq_excess[:, two], func=ACT.Abs_reciprocal_sqrt,
-                scale=SHRINK, bias=eps2_shrunk[:],
+                out=inv_norm[:, two], in_=row_sq[:, two], func=ACT.Abs_reciprocal_sqrt,
+                scale=SHRINK, bias=floor[:],
             )
 
         def clamp(c):
@@ -197,8 +193,8 @@ def tile_dispatcher_pa_s_kernel(tc, inv, Wk_words, Wk_scales, bk, out):
         def row_gain(c):
             two = slice(2 * c, 2 * c + 2)
             nc.vector.scalar_tensor_tensor(
-                out=gain[:, two], in0=inv_denom[:, two], scalar=-2.0 * math.sqrt(SHRINK) / EPS,
-                in1=row_sum[:, two], op0=ALU.mult, op1=ALU.mult,
+                out=gain[:, two], in0=inv_norm[:, two], scalar=1.0 / (EPS * math.sqrt(SHRINK)),
+                in1=row_sum[:, two], op0=ALU.min, op1=ALU.mult,
             )
 
         def scale_on_scalar(t):
@@ -359,7 +355,9 @@ def tile_dispatcher_pa_s_kernel(tc, inv, Wk_words, Wk_scales, bk, out):
         spread(1, 0, False, False)
         spread(0, 1, False, False)
         spread(1, 1, False, True)
-        nc.vector.tensor_copy(out=out_sb[:, 0 : 2 * P], in_=wide[:])
+        nc.vector.tensor_scalar(
+            out=out_sb[:, 0 : 2 * P], in0=wide[:], scalar1=UNIT, scalar2=None, op0=ALU.mult
+        )
         store(0)
         scalar_sum(2, 1)
         narrow = bank(2, P, "spread")
@@ -372,6 +370,11 @@ def tile_dispatcher_pa_s_kernel(tc, inv, Wk_words, Wk_scales, bk, out):
         spread(3, 0, False, False)
         spread(3, 1, False, True)
         spread(2, 1, False, True)
-        nc.vector.tensor_copy(out=out_sb[:, 3 * P : 4 * P], in_=spread_of[3])
-        nc.scalar.copy(out=out_sb[:, 2 * P : 3 * P], in_=spread_of[2])
+        nc.vector.tensor_scalar(
+            out=out_sb[:, 3 * P : 4 * P], in0=spread_of[3], scalar1=UNIT, scalar2=None,
+            op0=ALU.mult,
+        )
+        nc.scalar.activation(
+            out=out_sb[:, 2 * P : 3 * P], in_=spread_of[2], func=ACT.Copy, scale=UNIT
+        )
         store(1)

@@ -109,7 +109,8 @@ def tile_dispatcher_pa_s_kernel(tc, inv, Wk_words, Wk_scales, bk, out):
         planes = keep.tile([P, TILES * P], U8, align_bytes=64)
         bias_sb = const.tile([P, D], F32)
         z = keep.tile([P, TILES, D], F32)
-        z_clamped = keep.tile([P, TILES, D], F32)
+        clamped_even = keep.tile([P, 1, D], F32)
+        clamped_odd = keep.tile([P, PAIRS, D], F32)
         squares = keep.tile([P, TILES, D], F32)
         row_sum = keep.tile([P, TILES], F32)
         row_sq = keep.tile([P, TILES], F32)
@@ -183,12 +184,14 @@ def tile_dispatcher_pa_s_kernel(tc, inv, Wk_words, Wk_scales, bk, out):
                 scale=SHRINK, bias=floor[:],
             )
 
-        def clamp(c):
-            for t in (2 * c, 2 * c + 1):
-                nc.vector.tensor_scalar(
-                    out=z_clamped[:, t, :], in0=z[:, t, :], scalar1=CLAMP, scalar2=-CLAMP,
-                    op0=ALU.min, op1=ALU.max,
-                )
+        def clamped(t):
+            return clamped_odd[:, t // 2, :] if t % 2 else clamped_even[:, 0, :]
+
+        def clamp(t, engine):
+            engine.tensor_scalar(
+                out=clamped(t), in0=z[:, t, :], scalar1=CLAMP, scalar2=-CLAMP,
+                op0=ALU.min, op1=ALU.max,
+            )
 
         def row_gain(c):
             two = slice(2 * c, 2 * c + 2)
@@ -199,13 +202,13 @@ def tile_dispatcher_pa_s_kernel(tc, inv, Wk_words, Wk_scales, bk, out):
 
         def scale_on_scalar(t):
             nc.scalar.activation(
-                out=signed_c[:, t, :], in_=z_clamped[:, t, :], func=ACT.Copy,
+                out=signed_c[:, t, :], in_=clamped(t), func=ACT.Copy,
                 scale=gain[:, t : t + 1],
             )
 
         def scale(t):
             nc.vector.tensor_scalar(
-                out=signed_c[:, t, :], in0=z_clamped[:, t, :], scalar1=gain[:, t : t + 1],
+                out=signed_c[:, t, :], in0=clamped(t), scalar1=gain[:, t : t + 1],
                 scalar2=-1.0 if t % 2 == 0 else 1.0, op0=ALU.mult, op1=ALU.mult,
             )
 
@@ -297,6 +300,8 @@ def tile_dispatcher_pa_s_kernel(tc, inv, Wk_words, Wk_scales, bk, out):
         for s in range(PAIRS):
             for c in pairs_at(s + FLIP_LEAD):
                 flip(2 * c, 2)
+            for c in pairs_at(s - GAIN_LAG):
+                clamp(2 * c, nc.gpsimd)
             add_bias(2 * s)
             if s == 0:
                 quantise(2, 2)
@@ -312,7 +317,7 @@ def tile_dispatcher_pa_s_kernel(tc, inv, Wk_words, Wk_scales, bk, out):
             square(2 * s + 1)
             for c in pairs_at(s - GAIN_LAG):
                 row_gain(c)
-                clamp(c)
+                clamp(2 * c + 1, nc.vector)
                 if c == last - 1:
                     turn_shifted()
                 for t in (2 * c, 2 * c + 1):
@@ -323,8 +328,11 @@ def tile_dispatcher_pa_s_kernel(tc, inv, Wk_words, Wk_scales, bk, out):
                         scale(t)
                         turn(t)
             inverse_norm(s)
-        clamp(last)
+        for t in (TILES - 2, TILES - 1):
+            clamp(t, nc.vector)
         row_gain(last)
+        for t in waiting:
+            turn(t)
         for t in (TILES - 2, TILES - 1):
             scale(t)
         for block in (0, 1, 3, 2):

import math
from contextlib import ExitStack

import concourse.mybir as mybir
from concourse.masks import make_identity

F32 = mybir.dt.float32
BF16 = mybir.dt.bfloat16
I32 = mybir.dt.int32
U32 = mybir.dt.uint32
U8 = mybir.dt.uint8
FP8X4 = mybir.dt.float8_e4m3fn_x4
FP4X4 = mybir.dt.float4_e2m1fn_x4
ALU = mybir.AluOpType
ACT = mybir.ActivationFunctionType
AXIS = mybir.AxisListType

P = 128
ROWS = 1024
D = 512
EPS = 1e-8
TILES = ROWS // P
PAIRS = TILES // 2
BLOCKS = D // P
BANK = 512
CLAMP = EPS / math.sqrt(D)
SHRINK = 2.0 ** -16
FLOOR = 2.0 ** -86
UNIT = 2.0 * math.sqrt(SHRINK) / EPS

FLIP_LEAD = 2
PRODUCT_LEAD = 1
GAIN_LAG = 1

FLOPS = 2 * ROWS * D * D


def tile_dispatcher_pa_s_kernel(tc, inv, Wk_words, Wk_scales, bk, out):
    nc = tc.nc
    with ExitStack() as stack:
        const = stack.enter_context(tc.tile_pool(name="const", bufs=1))
        keep = stack.enter_context(tc.tile_pool(name="keep", bufs=1))
        psum = stack.enter_context(tc.psum_pool(name="psum", bufs=1))

        def bank(number, width, name):
            return psum.tile([P, width], F32, tag="bank%d" % number, name=name)

        stack.enter_context(tc.manual_schedule())

        rows = inv.flatten_outer_dims().rearrange("(p t) k -> p t k", t=TILES)
        x_sb = keep.tile([P, TILES, D], BF16)

        def load_pair(c):
            nc.sync.dma_start(out=x_sb[:, 2 * c : 2 * c + 2, :], in_=rows[:, 2 * c : 2 * c + 2, :])

        bias_row = const.tile([P, D], BF16)
        nc.gpsimd.memset(bias_row[:].bitcast(F32), 0.0)
        nc.scalar.dma_start(out=bias_row[0:1, :], in_=bk.rearrange("(o n) -> o n", o=1))
        load_pair(0)
        load_pair(1)
        w_plane = const.tile([P, D], U8, align_bytes=64)
        nc.vector.memset(w_plane[:].bitcast(I32), 0)
        scale_rows = Wk_scales.rearrange("g q n -> (g q) n")
        for quad in range(4):
            nc.sync.dma_start(
                out=w_plane[32 * quad : 32 * quad + 4, :].bitcast(I32),
                in_=scale_rows[4 * quad : 4 * quad + 4, :].bitcast(I32),
            )
        w_bytes = const.tile([P, 2 * D], U8, align_bytes=64)
        nc.sync.dma_start(
            out=w_bytes[:].bitcast(I32),
            in_=Wk_words.rearrange("g p n -> (g p) n").bitcast(I32),
        )
        load_pair(2)
        load_pair(3)

        floor = const.tile([P, 1], F32)
        nc.vector.memset(floor[:], FLOOR)
        warm = const.tile([P, 1], F32)
        nc.scalar.activation(out=warm[:], in_=floor[:], func=ACT.Abs_reciprocal_sqrt)
        idle_sb = const.tile([P, D], BF16)
        nc.vector.memset(idle_sb[:], 1.0)
        idle_ps = bank(5, D, "idle_ps")
        for width in (D, D // 2):
            nc.tensor.matmul(
                out=idle_ps[:, 0:width], lhsT=idle_sb[:, 0:P], rhs=idle_sb[:, 0:width],
                start=True, stop=True,
            )

        ident = const.tile([P, P], F32)
        make_identity(nc, ident[:])
        ends = const.tile([P, 2], F32)
        nc.vector.tensor_scalar(
            out=ends[:, 0:1], in0=ident[:, 0:1], scalar1=-0.5, scalar2=None, op0=ALU.mult
        )
        nc.vector.tensor_scalar(
            out=ends[:, 1:2], in0=ident[:, P - 1 : P], scalar1=-0.5, scalar2=None, op0=ALU.mult
        )
        ones = const.tile([P, P], BF16)
        nc.gpsimd.memset(ones[:], 1.0)
        shift_up = const.tile([P, P], F32)
        nc.vector.tensor_copy(out=shift_up[:, 0 : P - 1], in_=ident[:, 1:P])
        nc.vector.tensor_copy(out=shift_up[:, P - 1 : P], in_=ident[:, 0:1])

        x_words = x_sb[:].rearrange("p t k -> p (t k)").bitcast(F32)
        grouped = keep.tile([P, TILES * P * 4], BF16, align_bytes=64)
        grouped_words = grouped[:].bitcast(F32)
        codes = keep.tile([P, TILES * P], U32, align_bytes=64)
        planes = keep.tile([P, TILES * P], U8, align_bytes=64)
        bias_sb = const.tile([P, D], F32)
        z = keep.tile([P, TILES, D], F32)
        clamped_even = keep.tile([P, 1, D], F32)
        clamped_odd = keep.tile([P, PAIRS, D], F32)
        squares = keep.tile([P, TILES, D], F32)
        row_sum = keep.tile([P, TILES], F32)
        row_sq = keep.tile([P, TILES], F32)
        inv_norm = keep.tile([P, TILES], F32)
        gain = keep.tile([P, TILES], F32)
        signed_c = keep.tile([P, TILES, D], F32)
        written = keep.tile([P, TILES, BANK], F32)
        partial = keep.tile([P, BLOCKS, 2], F32)
        acc = {}
        turned = {}

        def flip(first, count):
            flipped = bank((first + 1) // 2 if first > 1 else first + 5, count * 2 * P, "flipped")
            for a in range(count):
                t = first + a
                for u in range(2):
                    nc.tensor.transpose(
                        flipped[:, (2 * a + u) * P : (2 * a + u + 1) * P],
                        x_words[:, t * (D // 2) + u : (t + 1) * (D // 2) : 2],
                        ident[:],
                    )
            nc.scalar.copy(
                out=grouped_words[:, 2 * first * P : 2 * (first + count) * P].rearrange(
                    "q (a r u) -> q a r u", a=count, u=2
                ),
                in_=flipped[:].rearrange("q (a u r) -> q a r u", a=count, u=2),
            )

        def quantise(first, count):
            cols = slice(first * P, (first + count) * P)
            nc.vector.quantize_mx(
                out=codes[:, cols].bitcast(FP8X4),
                scales=planes[:, cols],
                in_=grouped[:, 4 * first * P : 4 * (first + count) * P],
            )

        def spread_bias():
            bias_ps = bank(4, D, "bias_ps")
            nc.tensor.matmul(out=bias_ps[:], lhsT=ones[:], rhs=bias_row[:], start=True, stop=True)
            nc.vector.tensor_copy(out=bias_sb[:], in_=bias_ps[:])

        def product(c):
            for t in (2 * c, 2 * c + 1):
                acc[t] = bank((0, 6, 5, 7, 5, 6, 7, 5)[t], BANK, "acc")
                nc.tensor.matmul_mx(
                    out=acc[t][:],
                    lhsT=codes[:, t * P : (t + 1) * P].bitcast(FP8X4),
                    lhsT_scale=planes[:, t * P : (t + 1) * P],
                    rhs=w_bytes[:].bitcast(FP4X4),
                    rhs_scale=w_plane[:],
                    start=True,
                    stop=True,
                )

        def add_bias(t):
            nc.vector.scalar_tensor_tensor(
                out=z[:, t, :], in0=acc[t][:], scalar=1.0, in1=bias_sb[:],
                op0=ALU.mult, op1=ALU.add, accum_out=row_sum[:, t : t + 1],
            )

        def square(t):
            nc.scalar.activation(
                out=squares[:, t, :], in_=z[:, t, :], func=ACT.Square,
                accum_out=row_sq[:, t : t + 1],
            )

        def inverse_norm(c):
            two = slice(2 * c, 2 * c + 2)
            nc.scalar.activation(
                out=inv_norm[:, two], in_=row_sq[:, two], func=ACT.Abs_reciprocal_sqrt,
                scale=SHRINK, bias=floor[:],
            )

        def clamped(t):
            return clamped_odd[:, t // 2, :] if t % 2 else clamped_even[:, 0, :]

        def clamp(t, engine):
            engine.tensor_scalar(
                out=clamped(t), in0=z[:, t, :], scalar1=CLAMP, scalar2=-CLAMP,
                op0=ALU.min, op1=ALU.max,
            )

        def row_gain(c):
            two = slice(2 * c, 2 * c + 2)
            nc.vector.scalar_tensor_tensor(
                out=gain[:, two], in0=inv_norm[:, two], scalar=1.0 / (EPS * math.sqrt(SHRINK)),
                in1=row_sum[:, two], op0=ALU.min, op1=ALU.mult,
            )

        def scale_on_scalar(t):
            nc.scalar.activation(
                out=signed_c[:, t, :], in_=clamped(t), func=ACT.Copy,
                scale=gain[:, t : t + 1],
            )

        def scale(t):
            nc.vector.tensor_scalar(
                out=signed_c[:, t, :], in0=clamped(t), scalar1=gain[:, t : t + 1],
                scalar2=-1.0 if t % 2 == 0 else 1.0, op0=ALU.mult, op1=ALU.mult,
            )

        LAST_BLOCK = BLOCKS - 1

        def place(step, block):
            if block == LAST_BLOCK:
                return (block, step % 2), step // 2
            return (block, step // 4), step % 4

        bank_of = {}
        for block in range(LAST_BLOCK):
            bank_of[block, 0] = 1 + block
            bank_of[block, 1] = 5 + block
        bank_of[LAST_BLOCK, 0] = 4
        bank_of[LAST_BLOCK, 1] = 0
        count_left = {}

        def turn_into(step, block, t, moving):
            key, column = place(step, block)
            first = key not in turned
            if first:
                turned[key] = bank(bank_of[key], BANK, "turned")
                count_left[key] = 8
            count_left[key] -= 1
            nc.tensor.matmul(
                out=turned[key][:, column * P : (column + 1) * P],
                lhsT=signed_c[:, t, block * P : (block + 1) * P], rhs=moving,
                is_transpose=True, start=first, stop=count_left[key] == 0,
            )

        def turn(t):
            for block in range(BLOCKS):
                turn_block(t, block)

        def turn_block(t, block):
            if t > 0:
                turn_into(t - 1, block, t, ident[:])
            turn_into(t, block, t, ident[:])

        def turn_shifted():
            for block in range(BLOCKS):
                turn_into(TILES - 1, block, 0, shift_up[:])

        def scalar_sum(block, late):
            width = BANK - 1 if late else BANK
            nc.scalar.activation(
                out=written[:, 2 * block + late, 0:width], in_=turned[block, late][:, 0:width],
                func=ACT.Abs, scale=0.5,
                accum_out=partial[:, block, late : late + 1],
            )

        def vector_sum(key, width, positive, slot, block, which):
            nc.vector.tensor_scalar(
                out=written[:, slot, 0:width], in0=turned[key][:, 0:width],
                scalar1=0.0, scalar2=None, op0=ALU.max if positive else ALU.min,
                op1=ALU.add if positive else ALU.subtract,
                accum_out=partial[:, block, which : which + 1],
            )

        spread_of = {}

        def spread(block, column, first, last):
            nc.tensor.matmul(
                out=spread_of[block],
                lhsT=partial[:, block, column : column + 1].to_broadcast([P, P]), rhs=ident[:],
                is_transpose=True, start=first, stop=last,
            )

        def add_end(which, first):
            t = which * (TILES - 1)
            nc.tensor.matmul(
                out=spread_of[LAST_BLOCK], lhsT=ends[:, which : which + 1].to_broadcast([P, P]),
                rhs=signed_c[:, t, LAST_BLOCK * P :], start=first, stop=False,
            )

        def pairs_at(s):
            return [s] if 0 <= s < PAIRS else []

        last = PAIRS - 1
        flip(0, 1)
        quantise(0, 1)
        flip(1, 1)
        quantise(1, 1)
        spread_bias()
        flip(2, 2)
        product(0)
        waiting = []
        for s in range(PAIRS):
            for c in pairs_at(s + FLIP_LEAD):
                flip(2 * c, 2)
            for c in pairs_at(s - GAIN_LAG):
                clamp(2 * c, nc.gpsimd)
            add_bias(2 * s)
            if s == 0:
                quantise(2, 2)
                product(1)
            square(2 * s)
            if 0 < s < PAIRS - 1:
                quantise(2 * s + 2, 2)
                product(s + 1)
            for t in waiting:
                turn(t)
            waiting.clear()
            add_bias(2 * s + 1)
            square(2 * s + 1)
            for c in pairs_at(s - GAIN_LAG):
                row_gain(c)
                clamp(2 * c + 1, nc.vector)
                if c == last - 1:
                    turn_shifted()
                for t in (2 * c, 2 * c + 1):
                    if t in (1, 3):
                        scale_on_scalar(t)
                        waiting.append(t)
                    else:
                        scale(t)
                        turn(t)
            inverse_norm(s)
        for t in (TILES - 2, TILES - 1):
            clamp(t, nc.vector)
        row_gain(last)
        for t in waiting:
            turn(t)
        for t in (TILES - 2, TILES - 1):
            scale(t)
        for block in (0, 1, 3, 2):
            for t in (TILES - 2, TILES - 1):
                turn_block(t, block)
        scalar_sum(0, 0)
        scalar_sum(1, 0)
        scalar_sum(2, 0)
        scalar_sum(0, 1)
        scalar_sum(1, 1)
        vector_sum((LAST_BLOCK, 0), BANK, True, 6, LAST_BLOCK, 0)
        vector_sum((LAST_BLOCK, 1), BANK - 1, False, 7, LAST_BLOCK, 1)

        out_sb = keep.tile([P, D], F32)
        out_rows = out.rearrange("(e p) d -> p e d", p=P)

        def store(half):
            cols = slice(half * (D // 2), (half + 1) * (D // 2))
            nc.sync.dma_start(
                out=out_rows[:, :, cols],
                in_=out_sb[:, cols].unsqueeze(1).to_broadcast([P, D // P, D // 2]),
            )

        wide = bank(1, 2 * P, "spread")
        spread_of[0] = wide[:, 0:P]
        spread_of[1] = wide[:, P : 2 * P]
        spread(0, 0, True, False)
        spread(1, 0, False, False)
        spread(0, 1, False, False)
        spread(1, 1, False, True)
        nc.vector.tensor_scalar(
            out=out_sb[:, 0 : 2 * P], in0=wide[:], scalar1=UNIT, scalar2=None, op0=ALU.mult
        )
        store(0)
        scalar_sum(2, 1)
        narrow = bank(2, P, "spread")
        spread_of[3] = narrow[:]
        add_end(0, True)
        add_end(1, False)
        narrow = bank(3, P, "spread")
        spread_of[2] = narrow[:]
        spread(2, 0, True, False)
        spread(3, 0, False, False)
        spread(3, 1, False, True)
        spread(2, 1, False, True)
        nc.vector.tensor_scalar(
            out=out_sb[:, 3 * P : 4 * P], in0=spread_of[3], scalar1=UNIT, scalar2=None,
            op0=ALU.mult,
        )
        nc.scalar.activation(
            out=out_sb[:, 2 * P : 3 * P], in_=spread_of[2], func=ACT.Copy, scale=UNIT
        )
        store(1)
